import numpy as np
import ml_dtypes


def mxq(x, axis, fmt="e4m3"):
    dtype, down = {"e4m3": (ml_dtypes.float8_e4m3fn, 7), "e5m2": (ml_dtypes.float8_e5m2, 14)}[fmt]
    v = np.moveaxis(np.asarray(x, np.float32).astype(ml_dtypes.bfloat16).astype(np.float64), axis, -1)
    blocks = v.reshape(v.shape[:-1] + (-1, 32))
    amax = np.abs(blocks).max(-1, keepdims=True)
    byte = np.maximum(np.where(amax > 0, np.frexp(amax)[1] - 1 + 127, 0) - down, 1)
    scale = np.exp2(byte - 127.0)
    codes = (blocks / scale).astype(np.float32).astype(dtype).astype(np.float64)
    return np.moveaxis((codes * scale).reshape(v.shape), -1, axis)


WIDE = False


def mx_kscale(k):
    if not WIDE:
        return np.ones(k)
    levels = np.array([10, -10, 5, -5, 0])
    a = np.random.permutation(np.resize(levels, k // 512 * 4)).reshape(k // 512, 4)
    idx = np.arange(k)
    return np.exp2(a[idx // 512, idx % 128 // 32])


BF16 = ml_dtypes.bfloat16


def bf(x):
    return np.asarray(x, np.float32).astype(BF16)


def f64(x):
    return np.asarray(x).astype(np.float64)


E2M1 = np.array([0.0, 0.5, 1.0, 1.5, 2.0, 3.0, 4.0, 6.0, -0.0, -0.5, -1.0, -1.5, -2.0, -3.0, -4.0, -6.0])


def pack_weight(w, fmt):
    k, n = w.shape
    w = f64(bf(w)).reshape(k // 32, 32, n)
    amax = np.abs(w).max(1)
    if fmt == "e4m3":
        byte = np.frexp(amax)[1] - 1 + 127 - 7
    else:
        mant, ex = np.frexp(amax / 6.0)
        byte = np.where(mant > 0.5, ex, ex - 1) + 127
    byte = np.clip(np.where(amax > 0, byte, 1), 1, 254)
    scaled = (w * np.exp2(127.0 - byte)[:, None, :]).reshape(k, n).astype(np.float32)
    by_word = np.ascontiguousarray(scaled.reshape(k // 512, 128, 4, n).transpose(0, 1, 3, 2))
    if fmt == "e4m3":
        words = by_word.astype(ml_dtypes.float8_e4m3fn).view(np.uint8)
    else:
        c = by_word.astype(ml_dtypes.float4_e2m1fn).view(np.uint8) & 0xF
        words = c[..., 0::2] | (c[..., 1::2] << 4)
    return np.ascontiguousarray(words), np.ascontiguousarray(byte.astype(np.uint8).reshape(k // 512, 16, n))


def unpack_weight(words, scales, fmt):
    g, p, n, _ = words.shape
    if fmt == "e4m3":
        vals = np.ascontiguousarray(words).view(ml_dtypes.float8_e4m3fn).astype(np.float64)
    else:
        nib = np.empty((g, p, n, 4), np.uint8)
        nib[..., 0::2] = words & 0xF
        nib[..., 1::2] = words >> 4
        vals = E2M1[nib]
    vals = vals * np.repeat(np.exp2(scales.astype(np.float64) - 127.0), 8, axis=1)[..., None]
    return vals.transpose(0, 1, 3, 2).reshape(g * 512, n)

def pack4(w):
    words, scales = pack_weight(w, "e2m1")
    return words.reshape(words.shape[0], 128, -1), scales


def unpack4(words, scales):
    return unpack_weight(words.reshape(words.shape[0], 128, -1, 2), scales, "e2m1")


B, I, H = 2048, 512, 256
EPS = 1e-5


def sigmoid(v):
    return 1.0 / (1.0 + np.exp(-v))


def _bn(v, gamma, beta):
    m = np.mean(v, axis=0)
    var = np.var(v, axis=0)
    return (v - m) * (gamma / np.sqrt(var + EPS)) + beta


def setup_inputs():
    rn = np.random.standard_normal
    s = mx_kscale(I)
    x = bf(rn((B, I)) * s)
    c = bf(rn((B, H)))
    h = bf(rn((B, H)))
    w_ih_words, w_ih_scales = pack4((rn((4 * H, I)) / np.sqrt(I) / s).T)
    return {"x": x,
            "c": c,
            "h": h,
            "w_ih_words": w_ih_words,
            "w_ih_scales": w_ih_scales,
            "w_hh": bf(rn((4 * H, H)) / np.sqrt(H)),
            "b": bf(0.3 * rn(4 * H)),
            "g_ih": bf(1.0 + 0.1 * rn(4 * H)),
            "b_ih": bf(0.3 * rn(4 * H)),
            "g_hh": bf(1.0 + 0.1 * rn(4 * H)),
            "b_hh": bf(0.3 * rn(4 * H)),
            "g_c": bf(1.0 + 0.1 * rn(H)),
            "b_c": bf(0.3 * rn(H))}


def reference(x, c, h, w_ih_words, w_ih_scales, w_hh, b, g_ih, b_ih, g_hh, b_hh, g_c, b_c):
    ih = mxq(f64(x), 1, "e4m3") @ unpack4(w_ih_words, w_ih_scales)
    hh = f64(h) @ f64(w_hh).T
    ih = _bn(ih, f64(g_ih), f64(b_ih))
    hh = _bn(hh, f64(g_hh), f64(b_hh))
    gates = ih + hh + f64(b)
    f, i, o, g = np.split(gates, 4, axis=1)
    f = sigmoid(f)
    i = sigmoid(i)
    o = sigmoid(o)
    g = np.tanh(g)
    c_next = f * f64(c) + i * g
    c_next = _bn(c_next, f64(g_c), f64(b_c))
    h_next = o * np.tanh(c_next)
    return (c_next, h_next)

@@ -1,0 +1,366 @@
+from contextlib import ExitStack
+import math
+
+import concourse.mybir as mybir
+from concourse.masks import make_identity
+
+F32 = mybir.dt.float32
+BF16 = mybir.dt.bfloat16
+I32 = mybir.dt.int32
+U32 = mybir.dt.uint32
+U8 = mybir.dt.uint8
+FP8X4 = mybir.dt.float8_e4m3fn_x4
+FP4X4 = mybir.dt.float4_e2m1fn_x4
+ALU = mybir.AluOpType
+ACT = mybir.ActivationFunctionType
+AXIS = mybir.AxisListType
+
+P = 128
+BATCH = 2048
+N_IN = 512
+N_HID = 256
+N_GATES = 4 * N_HID
+EPS = 1e-5
+
+CHUNK = 512
+N_CHUNKS = BATCH // CHUNK
+ROW_TILES = BATCH // P
+TILES_PER_CHUNK = CHUNK // P
+K_TILES = N_HID // P
+HALVES = N_HID // P
+FORGET, IN, OUT, CELL = 0, 1, 2, 3
+
+HH_CHUNKS_ON_VECTOR = 1
+
+BANKS = {"hh": 4, "ih": 2, "tr": 2}
+
+FLOPS = 2 * BATCH * N_GATES * (N_IN + N_HID)
+
+
+def tile_lstmcell_kernel(
+    tc, x, c, h, w_ih_words, w_ih_scales, w_hh, b, g_ih, b_ih, g_hh, b_hh, g_c, b_c, out_0, out_1
+):
+    nc = tc.nc
+    with ExitStack() as ctx:
+        keep = ctx.enter_context(tc.tile_pool(name="keep", bufs=1))
+        psum = ctx.enter_context(tc.psum_pool(name="psum", bufs=1))
+
+        def bank(shape, dtype, tag):
+            return psum.tile(shape, dtype, name="bank_" + tag, tag=tag, bufs=BANKS[tag])
+
+        ident_bf = keep.tile([P, P], BF16, name="ident_bf")
+        make_identity(nc, ident_bf[:])
+        ident_f32 = keep.tile([P, P], F32, name="ident_f32")
+        make_identity(nc, ident_f32[:])
+        minus_half = keep.tile([P, 2], F32, name="minus_half")
+        nc.vector.memset(minus_half[:], -0.5)
+        eps2 = keep.tile([P, 2], F32, name="eps2")
+        nc.vector.memset(eps2[:, 0:1], EPS)
+        nc.vector.memset(eps2[:, 1:2], BATCH * EPS)
+        warm = keep.tile([P, 1], F32, name="warm")
+        nc.vector.memset(warm[:], 0.0)
+        nc.scalar.activation(out=warm[:], in_=warm[:], func=ACT.Sigmoid)
+
+        w_words = keep.tile([P, 2 * N_GATES], U8, name="w_words", align_bytes=64)
+        nc.sync.dma_start(out=w_words[:].bitcast(I32), in_=w_ih_words[0].bitcast(I32))
+        w_plane = keep.tile([P, N_GATES], U8, name="w_plane", align_bytes=64)
+        nc.vector.memset(w_plane[:].bitcast(I32), 0)
+        for quad in range(4):
+            nc.sync.dma_start(
+                out=w_plane[32 * quad : 32 * quad + 4, :].bitcast(I32),
+                in_=w_ih_scales[0, 4 * quad : 4 * quad + 4, :].bitcast(I32),
+            )
+
+        x_sb = keep.tile([P, ROW_TILES, N_IN], BF16, name="x_sb")
+        x_rows = x.rearrange("(p t) k -> p t k", t=ROW_TILES)
+        h_sb = keep.tile([P, ROW_TILES, N_HID], BF16, name="h_sb")
+        h_rows = h.rearrange("(p t) k -> p t k", t=ROW_TILES)
+        c_sb = keep.tile([P, ROW_TILES, N_HID], BF16, name="c_sb")
+        c_rows = c.rearrange("(p t) k -> p t k", t=ROW_TILES)
+        whh_sb = keep.tile([P, N_GATES // P, N_HID], BF16, name="whh_sb")
+
+        def load_chunk(dst, src, j):
+            tiles = slice(j * TILES_PER_CHUNK, (j + 1) * TILES_PER_CHUNK)
+            nc.sync.dma_start(out=dst[:, tiles, :], in_=src[:, tiles, :])
+
+        load_chunk(x_sb, x_rows, 0)
+        nc.sync.dma_start(out=whh_sb[:], in_=w_hh.rearrange("(a p) k -> p a k", p=P))
+        load_chunk(h_sb, h_rows, 0)
+        for j in range(1, N_CHUNKS):
+            load_chunk(x_sb, x_rows, j)
+            load_chunk(h_sb, h_rows, j)
+
+        par_rows = keep.tile([P, P], BF16, name="par_rows")
+        nc.vector.memset(par_rows[:], 0.0)
+        row = 0
+        for vec in (g_ih, g_hh, b, b_ih, b_hh, g_c, b_c):
+            n_rows = vec.shape[0] // P
+            nc.sync.dma_start(out=par_rows[row : row + n_rows, :], in_=vec.rearrange("(a j) -> a j", j=P))
+            row += n_rows
+        n_par = row
+        for j in range(N_CHUNKS):
+            load_chunk(c_sb, c_rows, j)
+
+        x_words = x_sb[:].rearrange("p t k -> p (t k)").bitcast(F32)
+        words_per_row = N_IN // 2
+        grouped = keep.tile([P, 4 * BATCH], BF16, name="grouped", align_bytes=64)
+        grouped_words = grouped[:].bitcast(F32).rearrange("p (col u) -> p col u", u=2)
+        xq_codes = keep.tile([P, BATCH], U32, name="xq_codes", align_bytes=64)
+        xq_plane = keep.tile([P, BATCH], U8, name="xq_plane", align_bytes=64)
+
+        def copy_out(i, out, in_):
+            if i % 2 == 0:
+                nc.vector.tensor_copy(out=out, in_=in_)
+            else:
+                nc.scalar.copy(out=out, in_=in_)
+
+        def transpose_x(j):
+            for pair in range(TILES_PER_CHUNK // 2):
+                first = j * TILES_PER_CHUNK + 2 * pair
+                xt = bank([P, 2, 2 * P], F32, "hh")
+                for u in range(2):
+                    for i in range(2):
+                        base = (first + i) * words_per_row
+                        nc.tensor.transpose(
+                            xt[:, u, i * P : (i + 1) * P],
+                            x_words[:, base + u : base + words_per_row : 2],
+                            ident_f32[:],
+                        )
+                copy_out(
+                    pair, grouped_words[:, first * P : (first + 2) * P, :], xt[:].rearrange("p u col -> p col u")
+                )
+
+        def quantise_x(j):
+            cols = slice(j * CHUNK, (j + 1) * CHUNK)
+            nc.vector.quantize_mx(
+                out=xq_codes[:, cols].bitcast(FP8X4),
+                scales=xq_plane[:, cols],
+                in_=grouped[:, 4 * j * CHUNK : 4 * (j + 1) * CHUNK],
+            )
+
+        whhT = keep.tile([P, K_TILES, N_GATES], BF16, name="whhT")
+        hT = keep.tile([P, K_TILES, BATCH], BF16, name="hT")
+        cT = keep.tile([P, HALVES, BATCH], BF16, name="cT")
+
+        def transpose_rows(dst, src, j):
+            for kt in range(K_TILES):
+                ps = bank([P, CHUNK], BF16, "tr")
+                for i in range(TILES_PER_CHUNK):
+                    nc.tensor.transpose(
+                        ps[:, i * P : (i + 1) * P], src[:, j * TILES_PER_CHUNK + i, kt * P : (kt + 1) * P], ident_bf[:]
+                    )
+                copy_out(kt, dst[:, kt, j * CHUNK : (j + 1) * CHUNK], ps[:])
+
+        transpose_x(0)
+        transpose_rows(whhT, whh_sb, 0)
+        transpose_rows(whhT, whh_sb, 1)
+        quantise_x(0)
+        transpose_rows(hT, h_sb, 0)
+        for j in range(1, N_CHUNKS):
+            transpose_x(j)
+            transpose_rows(hT, h_sb, j)
+            quantise_x(j)
+
+        par_ps = bank([P, P], BF16, "tr")
+        nc.tensor.transpose(par_ps[:], par_rows[:], ident_bf[:])
+        par = keep.tile([P, n_par], F32, name="par")
+        nc.vector.tensor_copy(out=par[:], in_=par_ps[:, 0:n_par])
+        n_ft = N_GATES // P
+        by_vec = par[:, 0 : 5 * n_ft].rearrange("p (v a) -> p v a", a=n_ft)
+        gain_c = par[:, 5 * n_ft : 5 * n_ft + HALVES]
+        offset_c = par[:, 5 * n_ft + HALVES : 5 * n_ft + 2 * HALVES]
+        offsets = keep.tile([P, n_ft], F32, name="offsets")
+        nc.vector.tensor_add(out=offsets[:], in0=by_vec[:, 2, :], in1=by_vec[:, 3, :])
+        nc.vector.tensor_add(out=offsets[:], in0=offsets[:], in1=by_vec[:, 4, :])
+        nc.vector.tensor_scalar(
+            out=by_vec[:, 1, :], in0=by_vec[:, 1, :], scalar1=math.sqrt(BATCH), scalar2=None, op0=ALU.mult
+        )
+
+        gate = [keep.tile([P, BATCH], F32, name="gate%d" % ft) for ft in range(n_ft)]
+        moments = [keep.tile([P, 2, 8], F32, name="moments%d" % ft) for ft in range(n_ft)]
+        slope = [keep.tile([P, 2], F32, name="slope%d" % ft) for ft in range(n_ft)]
+        shift = [keep.tile([P, 1], F32, name="shift%d" % ft) for ft in range(n_ft)]
+        squares = keep.tile([P, BATCH], BF16, name="squares")
+        scrap = keep.tile([P, N_CHUNKS], F32, name="scrap")
+        on_scalar = N_CHUNKS - HH_CHUNKS_ON_VECTOR
+        first_sum = 8 - on_scalar
+
+        def input_product(ft, j):
+            cols = slice(j * CHUNK, (j + 1) * CHUNK)
+            ih = bank([P, CHUNK], F32, "ih")
+            nc.tensor.matmul_mx(
+                out=ih[:],
+                lhsT=w_words[:, 2 * ft * P : 2 * (ft + 1) * P].bitcast(FP4X4),
+                lhsT_scale=w_plane[:, ft * P : (ft + 1) * P],
+                rhs=xq_codes[:, cols].bitcast(FP8X4),
+                rhs_scale=xq_plane[:, cols],
+                start=True,
+                stop=True,
+            )
+            return ih
+
+        def hidden_matmuls(ft):
+            banks = []
+            for j in range(N_CHUNKS):
+                hh = bank([P, CHUNK], F32, "hh")
+                for kt in range(K_TILES):
+                    nc.tensor.matmul(
+                        out=hh[:],
+                        lhsT=whhT[:, kt, ft * P : (ft + 1) * P],
+                        rhs=hT[:, kt, j * CHUNK : (j + 1) * CHUNK],
+                        start=(kt == 0),
+                        stop=(kt == K_TILES - 1),
+                    )
+                banks.append(hh)
+            return banks
+
+        def hidden_sums(ft, banks):
+            sums = keep.tile([P, 16], F32, name="sums%d" % ft)
+            for j in range(N_CHUNKS):
+                cols = slice(j * CHUNK, (j + 1) * CHUNK)
+                total = sums[:, first_sum + j : first_sum + j + 1]
+                if j < on_scalar:
+                    nc.scalar.activation(out=gate[ft][:, cols], in_=banks[j][:], func=ACT.Identity, accum_out=total)
+                else:
+                    nc.vector.tensor_scalar(
+                        out=gate[ft][:, cols], in0=banks[j][:], scalar1=1.0, scalar2=None,
+                        op0=ALU.mult, op1=ALU.add, accum_out=total,
+                    )
+            nc.scalar.activation(
+                out=scrap[:], in_=sums[:, first_sum : first_sum + N_CHUNKS], func=ACT.Identity,
+                scale=-1.0 / BATCH, accum_out=moments[ft][:, 1, 0:1],
+            )
+            nc.scalar.activation(
+                out=squares[:], in_=gate[ft][:], func=ACT.Square, bias=moments[ft][:, 1, 0:1],
+                accum_out=moments[ft][:, 1, 1:2],
+            )
+
+        def input_stats(ft):
+            stats = keep.tile([P, N_CHUNKS, 6], F32, name="stats%d" % ft)
+            for j in range(N_CHUNKS):
+                ih = input_product(ft, j)
+                nc.vector.bn_stats(out=stats[:, j, :], in_=ih[:])
+            nc.vector.bn_aggr(out=moments[ft][:, 0, 0:2], in_=stats[:].rearrange("p j s -> p (j s)"))
+
+        def inverse_std(out, variances):
+            width = out.shape[1]
+            nc.gpsimd.tensor_tensor(out=out, in0=variances, in1=eps2[:, 0:width], op=ALU.add)
+            nc.gpsimd.tensor_tensor(out=out, in0=out, in1=minus_half[:, 0:width], op=ALU.pow)
+
+        def coefficients(ft):
+            inverse_std(slope[ft][:], moments[ft][:, :, 1])
+            nc.gpsimd.tensor_tensor(out=slope[ft][:], in0=slope[ft][:], in1=by_vec[:, 0:2, ft], op=ALU.mult)
+            nc.gpsimd.tensor_scalar(
+                out=gate[ft][:], in0=gate[ft][:], scalar1=moments[ft][:, 1, 0:1], scalar2=slope[ft][:, 1:2],
+                op0=ALU.add, op1=ALU.mult,
+            )
+            nc.gpsimd.tensor_tensor(out=shift[ft][:], in0=slope[ft][:, 0:1], in1=moments[ft][:, 0, 0:1], op=ALU.mult)
+            nc.gpsimd.tensor_tensor(out=shift[ft][:], in0=offsets[:, ft : ft + 1], in1=shift[ft][:], op=ALU.subtract)
+
+        def apply(ft, func):
+            for j in range(N_CHUNKS):
+                cols = slice(j * CHUNK, (j + 1) * CHUNK)
+                ih = input_product(ft, j)
+                nc.vector.scalar_tensor_tensor(
+                    out=gate[ft][:, cols], in0=ih[:], scalar=slope[ft][:, 0:1], in1=gate[ft][:, cols],
+                    op0=ALU.mult, op1=ALU.add,
+                )
+            nc.scalar.activation(out=gate[ft][:], in_=gate[ft][:], func=func, bias=shift[ft][:])
+
+        def store(dram, half, src):
+            rows = dram.rearrange("(p t) f -> p t f", t=ROW_TILES)
+            staged = keep.tile([P, ROW_TILES, P], F32, name="staged", tag="staged", bufs=4)
+            for j in range(N_CHUNKS):
+                tiles = slice(j * TILES_PER_CHUNK, (j + 1) * TILES_PER_CHUNK)
+                ps = bank([P, TILES_PER_CHUNK, P], F32, "tr")
+                for i in range(TILES_PER_CHUNK):
+                    t = j * TILES_PER_CHUNK + i
+                    nc.tensor.transpose(ps[:, i, :], src[:, t * P : (t + 1) * P], ident_f32[:])
+                copy_out(j, staged[:, tiles, :], ps[:])
+                nc.sync.dma_start(out=rows[:, tiles, half * P : (half + 1) * P], in_=staged[:, tiles, :])
+
+        tanh_c = [keep.tile([P, BATCH], F32, name="tanh_c%d" % half) for half in range(HALVES)]
+        c_next = [keep.tile([P, BATCH], F32, name="c_next%d" % half) for half in range(HALVES)]
+        c_mean_var = [keep.tile([P, 2], F32, name="c_mean_var%d" % half) for half in range(HALVES)]
+        c_slope = [keep.tile([P, 1], F32, name="c_slope%d" % half) for half in range(HALVES)]
+        c_shift = [keep.tile([P, 1], F32, name="c_shift%d" % half) for half in range(HALVES)]
+
+        def tile_of(kind, half):
+            return HALVES * kind + half
+
+        def keep_old(half):
+            forget = gate[tile_of(FORGET, half)]
+            nc.gpsimd.tensor_tensor(out=forget[:], in0=forget[:], in1=cT[:, half, :], op=ALU.mult)
+
+        def take_new(half):
+            engine = nc.gpsimd if half < HALVES - 1 else nc.vector
+            in_gate = gate[tile_of(IN, half)]
+            engine.tensor_tensor(out=in_gate[:], in0=in_gate[:], in1=gate[tile_of(CELL, half)][:], op=ALU.mult)
+
+        def measure_cell(half):
+            raw, in_gate = gate[tile_of(FORGET, half)], gate[tile_of(IN, half)]
+            stats = keep.tile([P, N_CHUNKS, 6], F32, name="c_stats%d" % half)
+            for j in range(N_CHUNKS):
+                cols = slice(j * CHUNK, (j + 1) * CHUNK)
+                nc.vector.tensor_add(out=raw[:, cols], in0=raw[:, cols], in1=in_gate[:, cols])
+                nc.vector.bn_stats(out=stats[:, j, :], in_=raw[:, cols])
+            nc.vector.bn_aggr(out=c_mean_var[half][:], in_=stats[:].rearrange("p j s -> p (j s)"))
+            inverse_std(c_slope[half][:], c_mean_var[half][:, 1:2])
+            nc.gpsimd.tensor_tensor(
+                out=c_slope[half][:], in0=c_slope[half][:], in1=gain_c[:, half : half + 1], op=ALU.mult
+            )
+            nc.gpsimd.tensor_tensor(
+                out=c_shift[half][:], in0=c_slope[half][:], in1=c_mean_var[half][:, 0:1], op=ALU.mult
+            )
+            nc.gpsimd.tensor_tensor(
+                out=c_shift[half][:], in0=offset_c[:, half : half + 1], in1=c_shift[half][:], op=ALU.subtract
+            )
+
+        def finish_cell(half):
+            raw = gate[tile_of(FORGET, half)]
+            nc.vector.tensor_scalar(
+                out=c_next[half][:], in0=raw[:], scalar1=c_slope[half][:], scalar2=c_shift[half][:],
+                op0=ALU.mult, op1=ALU.add,
+            )
+            nc.scalar.activation(
+                out=tanh_c[half][:], in_=raw[:], func=ACT.Tanh, scale=c_slope[half][:], bias=c_shift[half][:]
+            )
+            store(out_0, half, c_next[half])
+
+        def finish_hidden(half):
+            h_next = gate[tile_of(OUT, half)]
+            nc.vector.tensor_mul(out=h_next[:], in0=h_next[:], in1=tanh_c[half][:])
+            store(out_1, half, h_next)
+
+        order = [(kind, half) for half in range(HALVES) for kind in (FORGET, IN, CELL)]
+        order += [(OUT, half) for half in range(HALVES)]
+        n = len(order)
+        tiles_in_order = [tile_of(kind, half) for kind, half in order]
+        funcs = [ACT.Tanh if kind == CELL else ACT.Sigmoid for kind, half in order]
+
+        banks = hidden_matmuls(tiles_in_order[0])
+        for s in range(n + 3):
+            if s < n:
+                hidden_sums(tiles_in_order[s], banks)
+            if 2 <= s < n + 2:
+                apply(tiles_in_order[s - 2], funcs[s - 2])
+            if s < n:
+                input_stats(tiles_in_order[s])
+            if s + 1 < n:
+                banks = hidden_matmuls(tiles_in_order[s + 1])
+            if 1 <= s < n + 1:
+                coefficients(tiles_in_order[s - 1])
+            if s < 2:
+                transpose_rows(cT, c_sb, 2 * s)
+                transpose_rows(cT, c_sb, 2 * s + 1)
+            for half in range(HALVES):
+                if s == order.index((FORGET, half)) + 4:
+                    keep_old(half)
+                if s == order.index((CELL, half)) + 3:
+                    take_new(half)
+                if s == order.index((CELL, half)) + 4:
+                    measure_cell(half)
+                if s == order.index((CELL, half)) + 5:
+                    finish_cell(half)
+                if s == max(order.index((OUT, half)) + 3, order.index((CELL, half)) + 5):
+                    finish_hidden(half)

@@ -13,7 +13,6 @@ FP8X4 = mybir.dt.float8_e4m3fn_x4
 FP4X4 = mybir.dt.float4_e2m1fn_x4
 ALU = mybir.AluOpType
 ACT = mybir.ActivationFunctionType
-AXIS = mybir.AxisListType
 
 P = 128
 BATCH = 2048
@@ -28,11 +27,12 @@ ROW_TILES = BATCH // P
 TILES_PER_CHUNK = CHUNK // P
 K_TILES = N_HID // P
 HALVES = N_HID // P
+N_TILES = N_GATES // P
 FORGET, IN, OUT, CELL = 0, 1, 2, 3
 
 HH_CHUNKS_ON_VECTOR = 1
 
-BANKS = {"hh": 4, "ih": 2, "tr": 2}
+BANKS = {"hh": 4, "ih": 4}
 
 FLOPS = 2 * BATCH * N_GATES * (N_IN + N_HID)
 
@@ -42,11 +42,15 @@ def tile_lstmcell_kernel(
 ):
     nc = tc.nc
     with ExitStack() as ctx:
+        ctx.enter_context(tc.manual_schedule())
         keep = ctx.enter_context(tc.tile_pool(name="keep", bufs=1))
         psum = ctx.enter_context(tc.psum_pool(name="psum", bufs=1))
 
         def bank(shape, dtype, tag):
             return psum.tile(shape, dtype, name="bank_" + tag, tag=tag, bufs=BANKS[tag])
+
+        def chunk(j):
+            return slice(j * CHUNK, (j + 1) * CHUNK)
 
         ident_bf = keep.tile([P, P], BF16, name="ident_bf")
         make_identity(nc, ident_bf[:])
@@ -61,6 +65,21 @@ def tile_lstmcell_kernel(
         nc.vector.memset(warm[:], 0.0)
         nc.scalar.activation(out=warm[:], in_=warm[:], func=ACT.Sigmoid)
 
+        x_sb = keep.tile([P, ROW_TILES, N_IN], BF16, name="x_sb")
+        x_rows = x.rearrange("(p t) k -> p t k", t=ROW_TILES)
+        h_sb = keep.tile([P, ROW_TILES, N_HID], BF16, name="h_sb")
+        h_rows = h.rearrange("(p t) k -> p t k", t=ROW_TILES)
+        c_sb = keep.tile([P, ROW_TILES, N_HID], BF16, name="c_sb")
+        c_rows = c.rearrange("(p t) k -> p t k", t=ROW_TILES)
+        whh_sb = keep.tile([P, N_TILES, N_HID], BF16, name="whh_sb")
+
+        def load_chunk(dst, src, j):
+            tiles = slice(j * TILES_PER_CHUNK, (j + 1) * TILES_PER_CHUNK)
+            nc.sync.dma_start(out=dst[:, tiles, :], in_=src[:, tiles, :])
+
+        for j in range(N_CHUNKS):
+            load_chunk(c_sb, c_rows, j)
+        load_chunk(x_sb, x_rows, 0)
         w_words = keep.tile([P, 2 * N_GATES], U8, name="w_words", align_bytes=64)
         nc.sync.dma_start(out=w_words[:].bitcast(I32), in_=w_ih_words[0].bitcast(I32))
         w_plane = keep.tile([P, N_GATES], U8, name="w_plane", align_bytes=64)
@@ -70,26 +89,11 @@ def tile_lstmcell_kernel(
                 out=w_plane[32 * quad : 32 * quad + 4, :].bitcast(I32),
                 in_=w_ih_scales[0, 4 * quad : 4 * quad + 4, :].bitcast(I32),
             )
-
-        x_sb = keep.tile([P, ROW_TILES, N_IN], BF16, name="x_sb")
-        x_rows = x.rearrange("(p t) k -> p t k", t=ROW_TILES)
-        h_sb = keep.tile([P, ROW_TILES, N_HID], BF16, name="h_sb")
-        h_rows = h.rearrange("(p t) k -> p t k", t=ROW_TILES)
-        c_sb = keep.tile([P, ROW_TILES, N_HID], BF16, name="c_sb")
-        c_rows = c.rearrange("(p t) k -> p t k", t=ROW_TILES)
-        whh_sb = keep.tile([P, N_GATES // P, N_HID], BF16, name="whh_sb")
-
-        def load_chunk(dst, src, j):
-            tiles = slice(j * TILES_PER_CHUNK, (j + 1) * TILES_PER_CHUNK)
-            nc.sync.dma_start(out=dst[:, tiles, :], in_=src[:, tiles, :])
-
-        load_chunk(x_sb, x_rows, 0)
         nc.sync.dma_start(out=whh_sb[:], in_=w_hh.rearrange("(a p) k -> p a k", p=P))
         load_chunk(h_sb, h_rows, 0)
         for j in range(1, N_CHUNKS):
             load_chunk(x_sb, x_rows, j)
             load_chunk(h_sb, h_rows, j)
-
         par_rows = keep.tile([P, P], BF16, name="par_rows")
         nc.vector.memset(par_rows[:], 0.0)
         row = 0
@@ -98,8 +102,6 @@ def tile_lstmcell_kernel(
             nc.sync.dma_start(out=par_rows[row : row + n_rows, :], in_=vec.rearrange("(a j) -> a j", j=P))
             row += n_rows
         n_par = row
-        for j in range(N_CHUNKS):
-            load_chunk(c_sb, c_rows, j)
 
         x_words = x_sb[:].rearrange("p t k -> p (t k)").bitcast(F32)
         words_per_row = N_IN // 2
@@ -131,10 +133,9 @@ def tile_lstmcell_kernel(
                 )
 
         def quantise_x(j):
-            cols = slice(j * CHUNK, (j + 1) * CHUNK)
             nc.vector.quantize_mx(
-                out=xq_codes[:, cols].bitcast(FP8X4),
-                scales=xq_plane[:, cols],
+                out=xq_codes[:, chunk(j)].bitcast(FP8X4),
+                scales=xq_plane[:, chunk(j)],
                 in_=grouped[:, 4 * j * CHUNK : 4 * (j + 1) * CHUNK],
             )
 
@@ -144,90 +145,65 @@ def tile_lstmcell_kernel(
 
         def transpose_rows(dst, src, j):
             for kt in range(K_TILES):
-                ps = bank([P, CHUNK], BF16, "tr")
+                ps = bank([P, CHUNK], BF16, "ih")
                 for i in range(TILES_PER_CHUNK):
                     nc.tensor.transpose(
                         ps[:, i * P : (i + 1) * P], src[:, j * TILES_PER_CHUNK + i, kt * P : (kt + 1) * P], ident_bf[:]
                     )
-                copy_out(kt, dst[:, kt, j * CHUNK : (j + 1) * CHUNK], ps[:])
+                copy_out(kt, dst[:, kt, chunk(j)], ps[:])
 
-        transpose_x(0)
-        transpose_rows(whhT, whh_sb, 0)
-        transpose_rows(whhT, whh_sb, 1)
-        quantise_x(0)
-        transpose_rows(hT, h_sb, 0)
-        for j in range(1, N_CHUNKS):
-            transpose_x(j)
-            transpose_rows(hT, h_sb, j)
-            quantise_x(j)
-
-        par_ps = bank([P, P], BF16, "tr")
-        nc.tensor.transpose(par_ps[:], par_rows[:], ident_bf[:])
-        par = keep.tile([P, n_par], F32, name="par")
-        nc.vector.tensor_copy(out=par[:], in_=par_ps[:, 0:n_par])
-        n_ft = N_GATES // P
-        by_vec = par[:, 0 : 5 * n_ft].rearrange("p (v a) -> p v a", a=n_ft)
-        gain_c = par[:, 5 * n_ft : 5 * n_ft + HALVES]
-        offset_c = par[:, 5 * n_ft + HALVES : 5 * n_ft + 2 * HALVES]
-        offsets = keep.tile([P, n_ft], F32, name="offsets")
-        nc.vector.tensor_add(out=offsets[:], in0=by_vec[:, 2, :], in1=by_vec[:, 3, :])
-        nc.vector.tensor_add(out=offsets[:], in0=offsets[:], in1=by_vec[:, 4, :])
-        nc.vector.tensor_scalar(
-            out=by_vec[:, 1, :], in0=by_vec[:, 1, :], scalar1=math.sqrt(BATCH), scalar2=None, op0=ALU.mult
-        )
-
-        gate = [keep.tile([P, BATCH], F32, name="gate%d" % ft) for ft in range(n_ft)]
-        moments = [keep.tile([P, 2, 8], F32, name="moments%d" % ft) for ft in range(n_ft)]
-        slope = [keep.tile([P, 2], F32, name="slope%d" % ft) for ft in range(n_ft)]
-        shift = [keep.tile([P, 1], F32, name="shift%d" % ft) for ft in range(n_ft)]
+        gate = [keep.tile([P, BATCH], F32, name="gate%d" % ft) for ft in range(N_TILES)]
+        moments = [keep.tile([P, 2, 8], F32, name="moments%d" % ft) for ft in range(N_TILES)]
+        stats = [keep.tile([P, N_CHUNKS, 6], F32, name="stats%d" % ft) for ft in range(N_TILES)]
+        sums = [keep.tile([P, 16], F32, name="sums%d" % ft) for ft in range(N_TILES)]
+        slope = [keep.tile([P, 2], F32, name="slope%d" % ft) for ft in range(N_TILES)]
+        shift = [keep.tile([P, 1], F32, name="shift%d" % ft) for ft in range(N_TILES)]
         squares = keep.tile([P, BATCH], BF16, name="squares")
         scrap = keep.tile([P, N_CHUNKS], F32, name="scrap")
         on_scalar = N_CHUNKS - HH_CHUNKS_ON_VECTOR
         first_sum = 8 - on_scalar
+        hh_banks = {}
 
         def input_product(ft, j):
-            cols = slice(j * CHUNK, (j + 1) * CHUNK)
             ih = bank([P, CHUNK], F32, "ih")
             nc.tensor.matmul_mx(
                 out=ih[:],
                 lhsT=w_words[:, 2 * ft * P : 2 * (ft + 1) * P].bitcast(FP4X4),
                 lhsT_scale=w_plane[:, ft * P : (ft + 1) * P],
-                rhs=xq_codes[:, cols].bitcast(FP8X4),
-                rhs_scale=xq_plane[:, cols],
+                rhs=xq_codes[:, chunk(j)].bitcast(FP8X4),
+                rhs_scale=xq_plane[:, chunk(j)],
                 start=True,
                 stop=True,
             )
             return ih
 
-        def hidden_matmuls(ft):
-            banks = []
-            for j in range(N_CHUNKS):
-                hh = bank([P, CHUNK], F32, "hh")
-                for kt in range(K_TILES):
-                    nc.tensor.matmul(
-                        out=hh[:],
-                        lhsT=whhT[:, kt, ft * P : (ft + 1) * P],
-                        rhs=hT[:, kt, j * CHUNK : (j + 1) * CHUNK],
-                        start=(kt == 0),
-                        stop=(kt == K_TILES - 1),
-                    )
-                banks.append(hh)
-            return banks
+        def hidden_pass(ft, i):
+            j, kt = i // K_TILES, i % K_TILES
+            if kt == 0:
+                hh_banks[(ft, j)] = bank([P, CHUNK], F32, "hh")
+            nc.tensor.matmul(
+                out=hh_banks[(ft, j)][:],
+                lhsT=whhT[:, kt, ft * P : (ft + 1) * P],
+                rhs=hT[:, kt, chunk(j)],
+                start=(kt == 0),
+                stop=(kt == K_TILES - 1),
+            )
 
-        def hidden_sums(ft, banks):
-            sums = keep.tile([P, 16], F32, name="sums%d" % ft)
-            for j in range(N_CHUNKS):
-                cols = slice(j * CHUNK, (j + 1) * CHUNK)
-                total = sums[:, first_sum + j : first_sum + j + 1]
-                if j < on_scalar:
-                    nc.scalar.activation(out=gate[ft][:, cols], in_=banks[j][:], func=ACT.Identity, accum_out=total)
-                else:
-                    nc.vector.tensor_scalar(
-                        out=gate[ft][:, cols], in0=banks[j][:], scalar1=1.0, scalar2=None,
-                        op0=ALU.mult, op1=ALU.add, accum_out=total,
-                    )
+        def hidden_out(ft, j):
+            total = sums[ft][:, first_sum + j : first_sum + j + 1]
+            if j < on_scalar:
+                nc.scalar.activation(
+                    out=gate[ft][:, chunk(j)], in_=hh_banks[(ft, j)][:], func=ACT.Identity, accum_out=total
+                )
+            else:
+                nc.vector.tensor_scalar(
+                    out=gate[ft][:, chunk(j)], in0=hh_banks[(ft, j)][:], scalar1=1.0, scalar2=None,
+                    op0=ALU.mult, op1=ALU.add, accum_out=total,
+                )
+
+        def hidden_moments(ft):
             nc.scalar.activation(
-                out=scrap[:], in_=sums[:, first_sum : first_sum + N_CHUNKS], func=ACT.Identity,
+                out=scrap[:], in_=sums[ft][:, first_sum : first_sum + N_CHUNKS], func=ACT.Identity,
                 scale=-1.0 / BATCH, accum_out=moments[ft][:, 1, 0:1],
             )
             nc.scalar.activation(
@@ -235,52 +211,44 @@ def tile_lstmcell_kernel(
                 accum_out=moments[ft][:, 1, 1:2],
             )
 
-        def input_stats(ft):
-            stats = keep.tile([P, N_CHUNKS, 6], F32, name="stats%d" % ft)
-            for j in range(N_CHUNKS):
-                ih = input_product(ft, j)
-                nc.vector.bn_stats(out=stats[:, j, :], in_=ih[:])
-            nc.vector.bn_aggr(out=moments[ft][:, 0, 0:2], in_=stats[:].rearrange("p j s -> p (j s)"))
+        def input_stats(ft, j):
+            ih = input_product(ft, j)
+            nc.vector.bn_stats(out=stats[ft][:, j, :], in_=ih[:])
+
+        def input_moments(ft):
+            nc.vector.bn_aggr(out=moments[ft][:, 0, 0:2], in_=stats[ft][:].rearrange("p j s -> p (j s)"))
 
         def inverse_std(out, variances):
             width = out.shape[1]
             nc.gpsimd.tensor_tensor(out=out, in0=variances, in1=eps2[:, 0:width], op=ALU.add)
             nc.gpsimd.tensor_tensor(out=out, in0=out, in1=minus_half[:, 0:width], op=ALU.pow)
 
-        def coefficients(ft):
+        def slopes(ft):
             inverse_std(slope[ft][:], moments[ft][:, :, 1])
             nc.gpsimd.tensor_tensor(out=slope[ft][:], in0=slope[ft][:], in1=by_vec[:, 0:2, ft], op=ALU.mult)
-            nc.gpsimd.tensor_scalar(
+
+        def norm_hidden(ft):
+            nc.vector.tensor_scalar(
                 out=gate[ft][:], in0=gate[ft][:], scalar1=moments[ft][:, 1, 0:1], scalar2=slope[ft][:, 1:2],
                 op0=ALU.add, op1=ALU.mult,
             )
-            nc.gpsimd.tensor_tensor(out=shift[ft][:], in0=slope[ft][:, 0:1], in1=moments[ft][:, 0, 0:1], op=ALU.mult)
-            nc.gpsimd.tensor_tensor(out=shift[ft][:], in0=offsets[:, ft : ft + 1], in1=shift[ft][:], op=ALU.subtract)
+            nc.vector.tensor_mul(out=shift[ft][:], in0=slope[ft][:, 0:1], in1=moments[ft][:, 0, 0:1])
+            nc.vector.tensor_sub(out=shift[ft][:], in0=offsets[:, ft : ft + 1], in1=shift[ft][:])
 
-        def apply(ft, func):
-            for j in range(N_CHUNKS):
-                cols = slice(j * CHUNK, (j + 1) * CHUNK)
-                ih = input_product(ft, j)
-                nc.vector.scalar_tensor_tensor(
-                    out=gate[ft][:, cols], in0=ih[:], scalar=slope[ft][:, 0:1], in1=gate[ft][:, cols],
-                    op0=ALU.mult, op1=ALU.add,
-                )
+        def add_input(ft, j):
+            ih = input_product(ft, j)
+            nc.vector.scalar_tensor_tensor(
+                out=gate[ft][:, chunk(j)], in0=ih[:], scalar=slope[ft][:, 0:1], in1=gate[ft][:, chunk(j)],
+                op0=ALU.mult, op1=ALU.add,
+            )
+
+        def activate(ft):
+            func = ACT.Tanh if ft // HALVES == CELL else ACT.Sigmoid
             nc.scalar.activation(out=gate[ft][:], in_=gate[ft][:], func=func, bias=shift[ft][:])
-
-        def store(dram, half, src):
-            rows = dram.rearrange("(p t) f -> p t f", t=ROW_TILES)
-            staged = keep.tile([P, ROW_TILES, P], F32, name="staged", tag="staged", bufs=4)
-            for j in range(N_CHUNKS):
-                tiles = slice(j * TILES_PER_CHUNK, (j + 1) * TILES_PER_CHUNK)
-                ps = bank([P, TILES_PER_CHUNK, P], F32, "tr")
-                for i in range(TILES_PER_CHUNK):
-                    t = j * TILES_PER_CHUNK + i
-                    nc.tensor.transpose(ps[:, i, :], src[:, t * P : (t + 1) * P], ident_f32[:])
-                copy_out(j, staged[:, tiles, :], ps[:])
-                nc.sync.dma_start(out=rows[:, tiles, half * P : (half + 1) * P], in_=staged[:, tiles, :])
 
         tanh_c = [keep.tile([P, BATCH], F32, name="tanh_c%d" % half) for half in range(HALVES)]
         c_next = [keep.tile([P, BATCH], F32, name="c_next%d" % half) for half in range(HALVES)]
+        c_stats = [keep.tile([P, N_CHUNKS, 6], F32, name="c_stats%d" % half) for half in range(HALVES)]
         c_mean_var = [keep.tile([P, 2], F32, name="c_mean_var%d" % half) for half in range(HALVES)]
         c_slope = [keep.tile([P, 1], F32, name="c_slope%d" % half) for half in range(HALVES)]
         c_shift = [keep.tile([P, 1], F32, name="c_shift%d" % half) for half in range(HALVES)]
@@ -293,18 +261,20 @@ def tile_lstmcell_kernel(
             nc.gpsimd.tensor_tensor(out=forget[:], in0=forget[:], in1=cT[:, half, :], op=ALU.mult)
 
         def take_new(half):
-            engine = nc.gpsimd if half < HALVES - 1 else nc.vector
             in_gate = gate[tile_of(IN, half)]
-            engine.tensor_tensor(out=in_gate[:], in0=in_gate[:], in1=gate[tile_of(CELL, half)][:], op=ALU.mult)
+            nc.gpsimd.tensor_tensor(out=in_gate[:], in0=in_gate[:], in1=gate[tile_of(CELL, half)][:], op=ALU.mult)
+
+        def sum_cell(half, engine):
+            raw = gate[tile_of(FORGET, half)]
+            engine.tensor_tensor(out=raw[:], in0=raw[:], in1=gate[tile_of(IN, half)][:], op=ALU.add)
 
         def measure_cell(half):
-            raw, in_gate = gate[tile_of(FORGET, half)], gate[tile_of(IN, half)]
-            stats = keep.tile([P, N_CHUNKS, 6], F32, name="c_stats%d" % half)
+            raw = gate[tile_of(FORGET, half)]
             for j in range(N_CHUNKS):
-                cols = slice(j * CHUNK, (j + 1) * CHUNK)
-                nc.vector.tensor_add(out=raw[:, cols], in0=raw[:, cols], in1=in_gate[:, cols])
-                nc.vector.bn_stats(out=stats[:, j, :], in_=raw[:, cols])
-            nc.vector.bn_aggr(out=c_mean_var[half][:], in_=stats[:].rearrange("p j s -> p (j s)"))
+                nc.vector.bn_stats(out=c_stats[half][:, j, :], in_=raw[:, chunk(j)])
+            nc.vector.bn_aggr(out=c_mean_var[half][:], in_=c_stats[half][:].rearrange("p j s -> p (j s)"))
+
+        def cell_slope(half):
             inverse_std(c_slope[half][:], c_mean_var[half][:, 1:2])
             nc.gpsimd.tensor_tensor(
                 out=c_slope[half][:], in0=c_slope[half][:], in1=gain_c[:, half : half + 1], op=ALU.mult
@@ -316,51 +286,130 @@ def tile_lstmcell_kernel(
                 out=c_shift[half][:], in0=offset_c[:, half : half + 1], in1=c_shift[half][:], op=ALU.subtract
             )
 
-        def finish_cell(half):
-            raw = gate[tile_of(FORGET, half)]
-            nc.vector.tensor_scalar(
-                out=c_next[half][:], in0=raw[:], scalar1=c_slope[half][:], scalar2=c_shift[half][:],
-                op0=ALU.mult, op1=ALU.add,
+        def norm_cell(half):
+            nc.gpsimd.tensor_scalar(
+                out=c_next[half][:], in0=gate[tile_of(FORGET, half)][:], scalar1=c_slope[half][:],
+                scalar2=c_shift[half][:], op0=ALU.mult, op1=ALU.add,
             )
+
+        def tanh_cell(half, j):
             nc.scalar.activation(
-                out=tanh_c[half][:], in_=raw[:], func=ACT.Tanh, scale=c_slope[half][:], bias=c_shift[half][:]
+                out=tanh_c[half][:, chunk(j)], in_=gate[tile_of(FORGET, half)][:, chunk(j)], func=ACT.Tanh,
+                scale=c_slope[half][:], bias=c_shift[half][:],
             )
-            store(out_0, half, c_next[half])
 
-        def finish_hidden(half):
+        def gate_hidden(half, j, engine):
             h_next = gate[tile_of(OUT, half)]
-            nc.vector.tensor_mul(out=h_next[:], in0=h_next[:], in1=tanh_c[half][:])
-            store(out_1, half, h_next)
+            engine.tensor_tensor(
+                out=h_next[:, chunk(j)], in0=h_next[:, chunk(j)], in1=tanh_c[half][:, chunk(j)], op=ALU.mult
+            )
 
-        order = [(kind, half) for half in range(HALVES) for kind in (FORGET, IN, CELL)]
-        order += [(OUT, half) for half in range(HALVES)]
-        n = len(order)
-        tiles_in_order = [tile_of(kind, half) for kind, half in order]
-        funcs = [ACT.Tanh if kind == CELL else ACT.Sigmoid for kind, half in order]
+        def store(dram, half, src, tag, first_copy):
+            rows = dram.rearrange("(p t) f -> p t f", t=ROW_TILES)
+            staged = keep.tile([P, ROW_TILES, P], F32, name="staged", tag="staged", bufs=4)
+            for j in range(N_CHUNKS):
+                tiles = slice(j * TILES_PER_CHUNK, (j + 1) * TILES_PER_CHUNK)
+                ps = bank([P, TILES_PER_CHUNK, P], F32, tag)
+                for i in range(TILES_PER_CHUNK):
+                    t = j * TILES_PER_CHUNK + i
+                    nc.tensor.transpose(ps[:, i, :], src[:, t * P : (t + 1) * P], ident_f32[:])
+                copy_out(first_copy(j), staged[:, tiles, :], ps[:])
+                nc.sync.dma_start(out=rows[:, tiles, half * P : (half + 1) * P], in_=staged[:, tiles, :])
 
-        banks = hidden_matmuls(tiles_in_order[0])
-        for s in range(n + 3):
-            if s < n:
-                hidden_sums(tiles_in_order[s], banks)
-            if 2 <= s < n + 2:
-                apply(tiles_in_order[s - 2], funcs[s - 2])
-            if s < n:
-                input_stats(tiles_in_order[s])
-            if s + 1 < n:
-                banks = hidden_matmuls(tiles_in_order[s + 1])
-            if 1 <= s < n + 1:
-                coefficients(tiles_in_order[s - 1])
-            if s < 2:
-                transpose_rows(cT, c_sb, 2 * s)
-                transpose_rows(cT, c_sb, 2 * s + 1)
-            for half in range(HALVES):
-                if s == order.index((FORGET, half)) + 4:
-                    keep_old(half)
-                if s == order.index((CELL, half)) + 3:
-                    take_new(half)
-                if s == order.index((CELL, half)) + 4:
-                    measure_cell(half)
-                if s == order.index((CELL, half)) + 5:
-                    finish_cell(half)
-                if s == max(order.index((OUT, half)) + 3, order.index((CELL, half)) + 5):
-                    finish_hidden(half)
+        def all_scalar(j):
+            return 1
+
+        def scalar_first(j):
+            return j + 1
+
+        order = [tile_of(kind, half) for half in range(HALVES) for kind in (FORGET, IN, CELL)]
+        order += [tile_of(OUT, half) for half in range(HALVES)]
+
+        def first_tile_chunk(j):
+            for kt in range(K_TILES):
+                hidden_pass(order[0], K_TILES * j + kt)
+            hidden_out(order[0], j)
+            input_stats(order[0], j)
+
+        for j in range(N_CHUNKS):
+            transpose_rows(cT, c_sb, j)
+        for j in range(N_CHUNKS):
+            transpose_x(j)
+            if j == 0:
+                transpose_rows(whhT, whh_sb, 0)
+                transpose_rows(whhT, whh_sb, 1)
+            transpose_rows(hT, h_sb, j)
+            quantise_x(j)
+            if j > 0:
+                first_tile_chunk(j - 1)
+
+        par_ps = bank([P, P], BF16, "ih")
+        nc.tensor.transpose(par_ps[:], par_rows[:], ident_bf[:])
+        par = keep.tile([P, n_par], F32, name="par")
+        nc.vector.tensor_copy(out=par[:], in_=par_ps[:, 0:n_par])
+        by_vec = par[:, 0 : 5 * N_TILES].rearrange("p (v a) -> p v a", a=N_TILES)
+        gain_c = par[:, 5 * N_TILES : 5 * N_TILES + HALVES]
+        offset_c = par[:, 5 * N_TILES + HALVES : 5 * N_TILES + 2 * HALVES]
+        offsets = keep.tile([P, N_TILES], F32, name="offsets")
+        nc.vector.tensor_add(out=offsets[:], in0=by_vec[:, 2, :], in1=by_vec[:, 3, :])
+        nc.vector.tensor_add(out=offsets[:], in0=offsets[:], in1=by_vec[:, 4, :])
+        nc.vector.tensor_scalar(
+            out=by_vec[:, 1, :], in0=by_vec[:, 1, :], scalar1=math.sqrt(BATCH), scalar2=None, op0=ALU.mult
+        )
+
+        first_tile_chunk(N_CHUNKS - 1)
+        hidden_moments(order[0])
+        input_moments(order[0])
+        for i in range(N_CHUNKS * K_TILES):
+            hidden_pass(order[1], i)
+
+        for s in range(1, N_TILES):
+            now, before = order[s], order[s - 1]
+            for j in range(N_CHUNKS):
+                hidden_out(now, j)
+            if s >= 2:
+                activate(order[s - 2])
+            hidden_moments(now)
+            slopes(before)
+            if s >= 3 and order[s - 3] // HALVES == FORGET:
+                keep_old(order[s - 3] % HALVES)
+            if s >= 2 and order[s - 2] // HALVES == CELL:
+                take_new(order[s - 2] % HALVES)
+            if s >= 3 and order[s - 3] // HALVES == CELL:
+                sum_cell(order[s - 3] % HALVES, nc.gpsimd)
+            for j in range(N_CHUNKS):
+                input_stats(now, j)
+                if s + 1 < N_TILES:
+                    hidden_pass(order[s + 1], j)
+            input_moments(now)
+            norm_hidden(before)
+            for j in range(N_CHUNKS):
+                add_input(before, j)
+                if s + 1 < N_TILES:
+                    hidden_pass(order[s + 1], N_CHUNKS + j)
+            if s >= 4 and order[s - 4] // HALVES == CELL:
+                measure_cell(order[s - 4] % HALVES)
+
+        activate(order[N_TILES - 2])
+        slopes(order[N_TILES - 1])
+        cell_slope(0)
+        norm_cell(0)
+        for j in range(N_CHUNKS):
+            tanh_cell(0, j)
+        for j in range(N_CHUNKS):
+            gate_hidden(0, j, nc.gpsimd)
+        norm_hidden(order[N_TILES - 1])
+        for j in range(N_CHUNKS):
+            add_input(order[N_TILES - 1], j)
+        sum_cell(1, nc.vector)
+        measure_cell(1)
+        cell_slope(1)
+        store(out_0, 0, c_next[0], "hh", all_scalar)
+        activate(order[N_TILES - 1])
+        store(out_1, 0, gate[tile_of(OUT, 0)], "ih", all_scalar)
+        norm_cell(1)
+        for j in range(N_CHUNKS):
+            tanh_cell(1, j)
+            gate_hidden(1, j, nc.vector)
+        store(out_1, 1, gate[tile_of(OUT, 1)], "hh", scalar_first)
+        store(out_0, 1, c_next[1], "ih", scalar_first)

@@ -227,13 +227,13 @@ def tile_lstmcell_kernel(
             inverse_std(slope[ft][:], moments[ft][:, :, 1])
             nc.gpsimd.tensor_tensor(out=slope[ft][:], in0=slope[ft][:], in1=by_vec[:, 0:2, ft], op=ALU.mult)
 
-        def norm_hidden(ft):
-            nc.vector.tensor_scalar(
+        def norm_hidden(ft, engine):
+            engine.tensor_scalar(
                 out=gate[ft][:], in0=gate[ft][:], scalar1=moments[ft][:, 1, 0:1], scalar2=slope[ft][:, 1:2],
                 op0=ALU.add, op1=ALU.mult,
             )
-            nc.vector.tensor_mul(out=shift[ft][:], in0=slope[ft][:, 0:1], in1=moments[ft][:, 0, 0:1])
-            nc.vector.tensor_sub(out=shift[ft][:], in0=offsets[:, ft : ft + 1], in1=shift[ft][:])
+            engine.tensor_tensor(out=shift[ft][:], in0=slope[ft][:, 0:1], in1=moments[ft][:, 0, 0:1], op=ALU.mult)
+            engine.tensor_tensor(out=shift[ft][:], in0=offsets[:, ft : ft + 1], in1=shift[ft][:], op=ALU.subtract)
 
         def add_input(ft, j):
             ih = input_product(ft, j)
@@ -260,9 +260,9 @@ def tile_lstmcell_kernel(
             forget = gate[tile_of(FORGET, half)]
             nc.gpsimd.tensor_tensor(out=forget[:], in0=forget[:], in1=cT[:, half, :], op=ALU.mult)
 
-        def take_new(half):
+        def take_new(half, engine):
             in_gate = gate[tile_of(IN, half)]
-            nc.gpsimd.tensor_tensor(out=in_gate[:], in0=in_gate[:], in1=gate[tile_of(CELL, half)][:], op=ALU.mult)
+            engine.tensor_tensor(out=in_gate[:], in0=in_gate[:], in1=gate[tile_of(CELL, half)][:], op=ALU.mult)
 
         def sum_cell(half, engine):
             raw = gate[tile_of(FORGET, half)]
@@ -304,23 +304,19 @@ def tile_lstmcell_kernel(
                 out=h_next[:, chunk(j)], in0=h_next[:, chunk(j)], in1=tanh_c[half][:, chunk(j)], op=ALU.mult
             )
 
-        def store(dram, half, src, tag, first_copy):
+        def flip(src, j, tag):
+            ps = bank([P, TILES_PER_CHUNK, P], F32, tag)
+            for i in range(TILES_PER_CHUNK):
+                t = j * TILES_PER_CHUNK + i
+                nc.tensor.transpose(ps[:, i, :], src[:, t * P : (t + 1) * P], ident_f32[:])
+            return ps
+
+        def unload(ps, j, dram, half, i):
             rows = dram.rearrange("(p t) f -> p t f", t=ROW_TILES)
-            staged = keep.tile([P, ROW_TILES, P], F32, name="staged", tag="staged", bufs=4)
-            for j in range(N_CHUNKS):
-                tiles = slice(j * TILES_PER_CHUNK, (j + 1) * TILES_PER_CHUNK)
-                ps = bank([P, TILES_PER_CHUNK, P], F32, tag)
-                for i in range(TILES_PER_CHUNK):
-                    t = j * TILES_PER_CHUNK + i
-                    nc.tensor.transpose(ps[:, i, :], src[:, t * P : (t + 1) * P], ident_f32[:])
-                copy_out(first_copy(j), staged[:, tiles, :], ps[:])
-                nc.sync.dma_start(out=rows[:, tiles, half * P : (half + 1) * P], in_=staged[:, tiles, :])
-
-        def all_scalar(j):
-            return 1
-
-        def scalar_first(j):
-            return j + 1
+            tiles = slice(j * TILES_PER_CHUNK, (j + 1) * TILES_PER_CHUNK)
+            staged = keep.tile([P, TILES_PER_CHUNK, P], F32, name="staged", tag="staged", bufs=8)
+            copy_out(i, staged[:], ps[:])
+            nc.sync.dma_start(out=rows[:, tiles, half * P : (half + 1) * P], in_=staged[:])
 
         order = [tile_of(kind, half) for half in range(HALVES) for kind in (FORGET, IN, CELL)]
         order += [tile_of(OUT, half) for half in range(HALVES)]
@@ -363,6 +359,9 @@ def tile_lstmcell_kernel(
         for i in range(N_CHUNKS * K_TILES):
             hidden_pass(order[1], i)
 
+        def kind_at(s):
+            return order[s] // HALVES if s >= 0 else None
+
         for s in range(1, N_TILES):
             now, before = order[s], order[s - 1]
             for j in range(N_CHUNKS):
@@ -371,45 +370,57 @@ def tile_lstmcell_kernel(
                 activate(order[s - 2])
             hidden_moments(now)
             slopes(before)
-            if s >= 3 and order[s - 3] // HALVES == FORGET:
-                keep_old(order[s - 3] % HALVES)
-            if s >= 2 and order[s - 2] // HALVES == CELL:
-                take_new(order[s - 2] % HALVES)
-            if s >= 3 and order[s - 3] // HALVES == CELL:
-                sum_cell(order[s - 3] % HALVES, nc.gpsimd)
+            if kind_at(s - 4) == FORGET:
+                keep_old(order[s - 4] % HALVES)
+            elif kind_at(s - 3) == CELL:
+                take_new(order[s - 3] % HALVES, nc.gpsimd)
+            elif kind_at(s - 4) == CELL:
+                sum_cell(order[s - 4] % HALVES, nc.gpsimd)
+            else:
+                norm_hidden(before, nc.gpsimd)
+            gpsimd_normed = kind_at(s - 4) not in (FORGET, CELL) and kind_at(s - 3) != CELL
             for j in range(N_CHUNKS):
                 input_stats(now, j)
                 if s + 1 < N_TILES:
                     hidden_pass(order[s + 1], j)
             input_moments(now)
-            norm_hidden(before)
+            if not gpsimd_normed:
+                norm_hidden(before, nc.vector)
             for j in range(N_CHUNKS):
                 add_input(before, j)
                 if s + 1 < N_TILES:
                     hidden_pass(order[s + 1], N_CHUNKS + j)
-            if s >= 4 and order[s - 4] // HALVES == CELL:
-                measure_cell(order[s - 4] % HALVES)
+            if kind_at(s - 5) == CELL:
+                measure_cell(order[s - 5] % HALVES)
 
+        last = order[N_TILES - 1]
         activate(order[N_TILES - 2])
-        slopes(order[N_TILES - 1])
+        slopes(last)
+        norm_hidden(last, nc.gpsimd)
         cell_slope(0)
         norm_cell(0)
+        take_new(1, nc.vector)
+        for j in range(N_CHUNKS):
+            add_input(last, j)
+        activate(last)
         for j in range(N_CHUNKS):
             tanh_cell(0, j)
-        for j in range(N_CHUNKS):
-            gate_hidden(0, j, nc.gpsimd)
-        norm_hidden(order[N_TILES - 1])
-        for j in range(N_CHUNKS):
-            add_input(order[N_TILES - 1], j)
         sum_cell(1, nc.vector)
         measure_cell(1)
         cell_slope(1)
-        store(out_0, 0, c_next[0], "hh", all_scalar)
-        activate(order[N_TILES - 1])
-        store(out_1, 0, gate[tile_of(OUT, 0)], "ih", all_scalar)
         norm_cell(1)
         for j in range(N_CHUNKS):
+            unload(flip(c_next[0], j, "hh"), j, out_0, 0, 1)
+        for j in range(N_CHUNKS):
+            gate_hidden(0, j, nc.vector)
+        flipped = [flip(gate[tile_of(OUT, 0)], j, "ih") for j in range(N_CHUNKS)]
+        for j in range(N_CHUNKS):
             tanh_cell(1, j)
+        for j in range(N_CHUNKS):
+            unload(flipped[j], j, out_1, 0, 0)
+        for j in range(N_CHUNKS):
             gate_hidden(1, j, nc.vector)
-        store(out_1, 1, gate[tile_of(OUT, 1)], "hh", scalar_first)
-        store(out_0, 1, c_next[1], "ih", scalar_first)
+        for j in range(N_CHUNKS):
+            unload(flip(gate[tile_of(OUT, 1)], j, "hh"), j, out_1, 1, j + 1)
+        for j in range(N_CHUNKS):
+            unload(flip(c_next[1], j, "ih"), j, out_0, 1, j + 1)

@@ -366,9 +366,9 @@ def tile_lstmcell_kernel(
             now, before = order[s], order[s - 1]
             for j in range(N_CHUNKS):
                 hidden_out(now, j)
+            hidden_moments(now)
             if s >= 2:
                 activate(order[s - 2])
-            hidden_moments(now)
             slopes(before)
             if kind_at(s - 4) == FORGET:
                 keep_old(order[s - 4] % HALVES)

@@ -20,6 +20,7 @@ N_IN = 512
 N_HID = 256
 N_GATES = 4 * N_HID
 EPS = 1e-5
+TINY_GAIN = 1e-18
 
 CHUNK = 512
 N_CHUNKS = BATCH // CHUNK
@@ -156,7 +157,11 @@ def tile_lstmcell_kernel(
         moments = [keep.tile([P, 2, 8], F32, name="moments%d" % ft) for ft in range(N_TILES)]
         stats = [keep.tile([P, N_CHUNKS, 6], F32, name="stats%d" % ft) for ft in range(N_TILES)]
         sums = [keep.tile([P, 16], F32, name="sums%d" % ft) for ft in range(N_TILES)]
+        spread = [keep.tile([P, 2], F32, name="spread%d" % ft) for ft in range(N_TILES)]
+        inv_std = [keep.tile([P, 2], F32, name="inv_std%d" % ft) for ft in range(N_TILES)]
         slope = [keep.tile([P, 2], F32, name="slope%d" % ft) for ft in range(N_TILES)]
+        ratio = [keep.tile([P, 1], F32, name="ratio%d" % ft) for ft in range(N_TILES)]
+        centre = [keep.tile([P, 1], F32, name="centre%d" % ft) for ft in range(N_TILES)]
         shift = [keep.tile([P, 1], F32, name="shift%d" % ft) for ft in range(N_TILES)]
         squares = keep.tile([P, BATCH], BF16, name="squares")
         scrap = keep.tile([P, N_CHUNKS], F32, name="scrap")
@@ -224,27 +229,34 @@ def tile_lstmcell_kernel(
             nc.gpsimd.tensor_tensor(out=out, in0=out, in1=minus_half[:, 0:width], op=ALU.pow)
 
         def slopes(ft):
-            inverse_std(slope[ft][:], moments[ft][:, :, 1])
-            nc.gpsimd.tensor_tensor(out=slope[ft][:], in0=slope[ft][:], in1=by_vec[:, 0:2, ft], op=ALU.mult)
-
-        def norm_hidden(ft, engine):
-            engine.tensor_scalar(
-                out=gate[ft][:], in0=gate[ft][:], scalar1=moments[ft][:, 1, 0:1], scalar2=slope[ft][:, 1:2],
-                op0=ALU.add, op1=ALU.mult,
+            nc.gpsimd.tensor_tensor(out=spread[ft][:], in0=moments[ft][:, :, 1], in1=eps2[:], op=ALU.add)
+            nc.gpsimd.tensor_tensor(out=inv_std[ft][:], in0=spread[ft][:], in1=minus_half[:], op=ALU.pow)
+            nc.gpsimd.tensor_tensor(out=slope[ft][:], in0=inv_std[ft][:], in1=by_vec[:, 0:2, ft], op=ALU.mult)
+            nc.gpsimd.tensor_scalar(
+                out=ratio[ft][:], in0=slope[ft][:, 0:1], scalar1=spread[ft][:, 1:2], scalar2=inv_std[ft][:, 1:2],
+                op0=ALU.mult, op1=ALU.mult,
             )
-            engine.tensor_tensor(out=shift[ft][:], in0=slope[ft][:, 0:1], in1=moments[ft][:, 0, 0:1], op=ALU.mult)
-            engine.tensor_tensor(out=shift[ft][:], in0=offsets[:, ft : ft + 1], in1=shift[ft][:], op=ALU.subtract)
+
+        def shifts(ft):
+            nc.gpsimd.tensor_scalar(
+                out=centre[ft][:], in0=moments[ft][:, 0, 0:1], scalar1=ratio[ft][:], scalar2=moments[ft][:, 1, 0:1],
+                op0=ALU.mult, op1=ALU.subtract,
+            )
+            nc.gpsimd.tensor_tensor(out=centre[ft][:], in0=centre[ft][:], in1=slope[ft][:, 1:2], op=ALU.mult)
+            nc.gpsimd.tensor_tensor(out=shift[ft][:], in0=offsets[:, ft : ft + 1], in1=centre[ft][:], op=ALU.subtract)
 
         def add_input(ft, j):
             ih = input_product(ft, j)
             nc.vector.scalar_tensor_tensor(
-                out=gate[ft][:, chunk(j)], in0=ih[:], scalar=slope[ft][:, 0:1], in1=gate[ft][:, chunk(j)],
+                out=gate[ft][:, chunk(j)], in0=ih[:], scalar=ratio[ft][:], in1=gate[ft][:, chunk(j)],
                 op0=ALU.mult, op1=ALU.add,
             )
 
         def activate(ft):
             func = ACT.Tanh if ft // HALVES == CELL else ACT.Sigmoid
-            nc.scalar.activation(out=gate[ft][:], in_=gate[ft][:], func=func, bias=shift[ft][:])
+            nc.scalar.activation(
+                out=gate[ft][:], in_=gate[ft][:], func=func, scale=slope[ft][:, 1:2], bias=shift[ft][:]
+            )
 
         tanh_c = [keep.tile([P, BATCH], F32, name="tanh_c%d" % half) for half in range(HALVES)]
         c_next = [keep.tile([P, BATCH], F32, name="c_next%d" % half) for half in range(HALVES)]
@@ -349,9 +361,17 @@ def tile_lstmcell_kernel(
         offsets = keep.tile([P, N_TILES], F32, name="offsets")
         nc.vector.tensor_add(out=offsets[:], in0=by_vec[:, 2, :], in1=by_vec[:, 3, :])
         nc.vector.tensor_add(out=offsets[:], in0=offsets[:], in1=by_vec[:, 4, :])
+        small = keep.tile([P, N_TILES], F32, name="small")
+        nc.vector.tensor_tensor(out=small[:], in0=by_vec[:, 1, :], in1=by_vec[:, 1, :], op=ALU.mult)
+        nc.vector.tensor_scalar(
+            out=small[:], in0=small[:], scalar1=TINY_GAIN * TINY_GAIN, scalar2=TINY_GAIN, op0=ALU.is_lt, op1=ALU.mult
+        )
+        nc.vector.tensor_tensor(out=by_vec[:, 1, :], in0=by_vec[:, 1, :], in1=small[:], op=ALU.add)
         nc.vector.tensor_scalar(
             out=by_vec[:, 1, :], in0=by_vec[:, 1, :], scalar1=math.sqrt(BATCH), scalar2=None, op0=ALU.mult
         )
+        nc.vector.reciprocal(out=small[:], in_=by_vec[:, 1, :])
+        nc.vector.tensor_tensor(out=by_vec[:, 0, :], in0=by_vec[:, 0, :], in1=small[:], op=ALU.mult)
 
         first_tile_chunk(N_CHUNKS - 1)
         hidden_moments(order[0])
@@ -370,22 +390,18 @@ def tile_lstmcell_kernel(
             if s >= 2:
                 activate(order[s - 2])
             slopes(before)
+            shifts(before)
             if kind_at(s - 4) == FORGET:
                 keep_old(order[s - 4] % HALVES)
             elif kind_at(s - 3) == CELL:
                 take_new(order[s - 3] % HALVES, nc.gpsimd)
             elif kind_at(s - 4) == CELL:
                 sum_cell(order[s - 4] % HALVES, nc.gpsimd)
-            else:
-                norm_hidden(before, nc.gpsimd)
-            gpsimd_normed = kind_at(s - 4) not in (FORGET, CELL) and kind_at(s - 3) != CELL
             for j in range(N_CHUNKS):
                 input_stats(now, j)
                 if s + 1 < N_TILES:
                     hidden_pass(order[s + 1], j)
             input_moments(now)
-            if not gpsimd_normed:
-                norm_hidden(before, nc.vector)
             for j in range(N_CHUNKS):
                 add_input(before, j)
                 if s + 1 < N_TILES:
@@ -396,7 +412,7 @@ def tile_lstmcell_kernel(
         last = order[N_TILES - 1]
         activate(order[N_TILES - 2])
         slopes(last)
-        norm_hidden(last, nc.gpsimd)
+        shifts(last)
         cell_slope(0)
         norm_cell(0)
         take_new(1, nc.vector)

@@ -31,9 +31,32 @@ HALVES = N_HID // P
 N_TILES = N_GATES // P
 FORGET, IN, OUT, CELL = 0, 1, 2, 3
 
+BANKS = {"v": 4, "s": 4}
+
 HH_CHUNKS_ON_VECTOR = 1
 
-BANKS = {"hh": 4, "ih": 4}
+ORDER = [(IN, 0), (CELL, 0), (FORGET, 0), (IN, 1), (CELL, 1), (FORGET, 1), (OUT, 0), (OUT, 1)]
+
+
+def PLAN(at, each_chunk, pos, tile_of, take_new, keep_old, sum_cell, measure_cell, cell_moments, cell_slope,
+         norm_cell, tanh_cell, gate_hidden, store, nc, gate, c_next, out_0, out_1, stage_hidden, store_hidden):
+    at(2, "mid", lambda: each_chunk(lambda j: take_new(0, j, nc.gpsimd)))
+    at(4, "mid", lambda: each_chunk(lambda j: keep_old(0, j), lambda j: sum_cell(0, j, nc.gpsimd)))
+    at(5, "mid", lambda: (each_chunk(lambda j: measure_cell(0, j)), cell_moments(0), cell_slope(0)))
+    at(5, "end", lambda: each_chunk(lambda j: take_new(1, j, nc.gpsimd)))
+    at(6, "end", lambda: each_chunk(lambda j: keep_old(1, j), lambda j: sum_cell(1, j, nc.gpsimd)))
+    at(7, "mid", lambda: each_chunk(lambda j: tanh_cell(0, j)))
+    at(7, "mid", lambda: each_chunk(lambda j: norm_cell(0, j, nc.scalar)))
+    at(7, "end", lambda: (each_chunk(lambda j: measure_cell(1, j)), cell_moments(1), cell_slope(1)))
+    at(7, "end", lambda: each_chunk(lambda j: store(c_next[0], j, out_0, 0, "s")))
+    at(8, "mid", lambda: each_chunk(lambda j: gate_hidden(0, j, nc.vector)))
+    at(8, "mid", lambda: each_chunk(lambda j: tanh_cell(1, j)))
+    at(8, "mid", lambda: each_chunk(lambda j: norm_cell(1, j, nc.vector)))
+    at(8, "mid", lambda: each_chunk(lambda j: gate_hidden(1, j, nc.vector)))
+    at(8, "mid", lambda: each_chunk(lambda j: store(gate[tile_of(OUT, 0)], j, out_1, 0, "s")))
+    at(8, "mid", lambda: each_chunk(lambda j: store(c_next[1], j, out_0, 1, "v")))
+    at(8, "mid", lambda: each_chunk(lambda j: store(gate[tile_of(OUT, 1)], j, out_1, 1, "svsv"[j])))
+
 
 FLOPS = 2 * BATCH * N_GATES * (N_IN + N_HID)
 
@@ -47,11 +70,17 @@ def tile_lstmcell_kernel(
         keep = ctx.enter_context(tc.tile_pool(name="keep", bufs=1))
         psum = ctx.enter_context(tc.psum_pool(name="psum", bufs=1))
 
-        def bank(shape, dtype, tag):
-            return psum.tile(shape, dtype, name="bank_" + tag, tag=tag, bufs=BANKS[tag])
+        def bank(shape, dtype, reader):
+            return psum.tile(shape, dtype, name="bank_" + reader, tag=reader, bufs=BANKS[reader])
 
         def chunk(j):
             return slice(j * CHUNK, (j + 1) * CHUNK)
+
+        def copy_out(reader, out, in_):
+            if reader == "v":
+                nc.vector.tensor_copy(out=out, in_=in_)
+            else:
+                nc.scalar.copy(out=out, in_=in_)
 
         ident_bf = keep.tile([P, P], BF16, name="ident_bf")
         make_identity(nc, ident_bf[:])
@@ -73,36 +102,39 @@ def tile_lstmcell_kernel(
         c_sb = keep.tile([P, ROW_TILES, N_HID], BF16, name="c_sb")
         c_rows = c.rearrange("(p t) k -> p t k", t=ROW_TILES)
         whh_sb = keep.tile([P, N_TILES, N_HID], BF16, name="whh_sb")
+        whh_rows = w_hh.rearrange("(a p) k -> p a k", p=P)
 
         def load_chunk(dst, src, j):
             tiles = slice(j * TILES_PER_CHUNK, (j + 1) * TILES_PER_CHUNK)
             nc.sync.dma_start(out=dst[:, tiles, :], in_=src[:, tiles, :])
 
-        for j in range(N_CHUNKS):
-            load_chunk(c_sb, c_rows, j)
-        load_chunk(x_sb, x_rows, 0)
-        w_words = keep.tile([P, 2 * N_GATES], U8, name="w_words", align_bytes=64)
-        nc.sync.dma_start(out=w_words[:].bitcast(I32), in_=w_ih_words[0].bitcast(I32))
+        par_rows = keep.tile([P, P], BF16, name="par_rows")
+        nc.vector.memset(par_rows[:], 0.0)
         w_plane = keep.tile([P, N_GATES], U8, name="w_plane", align_bytes=64)
         nc.vector.memset(w_plane[:].bitcast(I32), 0)
+
+        w_words = keep.tile([P, 2 * N_GATES], U8, name="w_words", align_bytes=64)
+        load_chunk(x_sb, x_rows, 0)
+        nc.sync.dma_start(out=w_words[:].bitcast(I32), in_=w_ih_words[0].bitcast(I32))
         for quad in range(4):
             nc.sync.dma_start(
                 out=w_plane[32 * quad : 32 * quad + 4, :].bitcast(I32),
                 in_=w_ih_scales[0, 4 * quad : 4 * quad + 4, :].bitcast(I32),
             )
-        nc.sync.dma_start(out=whh_sb[:], in_=w_hh.rearrange("(a p) k -> p a k", p=P))
-        load_chunk(h_sb, h_rows, 0)
+        for j in range(2):
+            load_chunk(whh_sb, whh_rows, j)
+        for j in range(N_CHUNKS):
+            load_chunk(h_sb, h_rows, j)
         for j in range(1, N_CHUNKS):
             load_chunk(x_sb, x_rows, j)
-            load_chunk(h_sb, h_rows, j)
-        par_rows = keep.tile([P, P], BF16, name="par_rows")
-        nc.vector.memset(par_rows[:], 0.0)
         row = 0
         for vec in (g_ih, g_hh, b, b_ih, b_hh, g_c, b_c):
             n_rows = vec.shape[0] // P
             nc.sync.dma_start(out=par_rows[row : row + n_rows, :], in_=vec.rearrange("(a j) -> a j", j=P))
             row += n_rows
         n_par = row
+        for j in range(N_CHUNKS):
+            load_chunk(c_sb, c_rows, j)
 
         x_words = x_sb[:].rearrange("p t k -> p (t k)").bitcast(F32)
         words_per_row = N_IN // 2
@@ -111,16 +143,10 @@ def tile_lstmcell_kernel(
         xq_codes = keep.tile([P, BATCH], U32, name="xq_codes", align_bytes=64)
         xq_plane = keep.tile([P, BATCH], U8, name="xq_plane", align_bytes=64)
 
-        def copy_out(i, out, in_):
-            if i % 2 == 0:
-                nc.vector.tensor_copy(out=out, in_=in_)
-            else:
-                nc.scalar.copy(out=out, in_=in_)
-
-        def transpose_x(j):
+        def transpose_x(j, readers):
             for pair in range(TILES_PER_CHUNK // 2):
                 first = j * TILES_PER_CHUNK + 2 * pair
-                xt = bank([P, 2, 2 * P], F32, "hh")
+                xt = bank([P, 2, 2 * P], F32, readers[pair])
                 for u in range(2):
                     for i in range(2):
                         base = (first + i) * words_per_row
@@ -130,7 +156,9 @@ def tile_lstmcell_kernel(
                             ident_f32[:],
                         )
                 copy_out(
-                    pair, grouped_words[:, first * P : (first + 2) * P, :], xt[:].rearrange("p u col -> p col u")
+                    readers[pair],
+                    grouped_words[:, first * P : (first + 2) * P, :],
+                    xt[:].rearrange("p u col -> p col u"),
                 )
 
         def quantise_x(j):
@@ -142,16 +170,15 @@ def tile_lstmcell_kernel(
 
         whhT = keep.tile([P, K_TILES, N_GATES], BF16, name="whhT")
         hT = keep.tile([P, K_TILES, BATCH], BF16, name="hT")
-        cT = keep.tile([P, HALVES, BATCH], BF16, name="cT")
 
-        def transpose_rows(dst, src, j):
+        def transpose_rows(dst, src, j, readers):
             for kt in range(K_TILES):
-                ps = bank([P, CHUNK], BF16, "ih")
+                ps = bank([P, CHUNK], BF16, readers[kt])
                 for i in range(TILES_PER_CHUNK):
                     nc.tensor.transpose(
                         ps[:, i * P : (i + 1) * P], src[:, j * TILES_PER_CHUNK + i, kt * P : (kt + 1) * P], ident_bf[:]
                     )
-                copy_out(kt, dst[:, kt, chunk(j)], ps[:])
+                copy_out(readers[kt], dst[:, kt, chunk(j)], ps[:])
 
         gate = [keep.tile([P, BATCH], F32, name="gate%d" % ft) for ft in range(N_TILES)]
         moments = [keep.tile([P, 2, 8], F32, name="moments%d" % ft) for ft in range(N_TILES)]
@@ -165,12 +192,11 @@ def tile_lstmcell_kernel(
         shift = [keep.tile([P, 1], F32, name="shift%d" % ft) for ft in range(N_TILES)]
         squares = keep.tile([P, BATCH], BF16, name="squares")
         scrap = keep.tile([P, N_CHUNKS], F32, name="scrap")
-        on_scalar = N_CHUNKS - HH_CHUNKS_ON_VECTOR
-        first_sum = 8 - on_scalar
         hh_banks = {}
+        hh_reader = {}
 
         def input_product(ft, j):
-            ih = bank([P, CHUNK], F32, "ih")
+            ih = bank([P, CHUNK], F32, "v")
             nc.tensor.matmul_mx(
                 out=ih[:],
                 lhsT=w_words[:, 2 * ft * P : 2 * (ft + 1) * P].bitcast(FP4X4),
@@ -185,7 +211,7 @@ def tile_lstmcell_kernel(
         def hidden_pass(ft, i):
             j, kt = i // K_TILES, i % K_TILES
             if kt == 0:
-                hh_banks[(ft, j)] = bank([P, CHUNK], F32, "hh")
+                hh_banks[(ft, j)] = bank([P, CHUNK], F32, hh_reader[(ft, j)])
             nc.tensor.matmul(
                 out=hh_banks[(ft, j)][:],
                 lhsT=whhT[:, kt, ft * P : (ft + 1) * P],
@@ -195,8 +221,8 @@ def tile_lstmcell_kernel(
             )
 
         def hidden_out(ft, j):
-            total = sums[ft][:, first_sum + j : first_sum + j + 1]
-            if j < on_scalar:
+            total = sums[ft][:, 4 + j : 5 + j]
+            if hh_reader[(ft, j)] == "s":
                 nc.scalar.activation(
                     out=gate[ft][:, chunk(j)], in_=hh_banks[(ft, j)][:], func=ACT.Identity, accum_out=total
                 )
@@ -206,11 +232,13 @@ def tile_lstmcell_kernel(
                     op0=ALU.mult, op1=ALU.add, accum_out=total,
                 )
 
-        def hidden_moments(ft):
+        def hidden_mean(ft):
             nc.scalar.activation(
-                out=scrap[:], in_=sums[ft][:, first_sum : first_sum + N_CHUNKS], func=ACT.Identity,
+                out=scrap[:], in_=sums[ft][:, 4 : 4 + N_CHUNKS], func=ACT.Identity,
                 scale=-1.0 / BATCH, accum_out=moments[ft][:, 1, 0:1],
             )
+
+        def hidden_spread(ft):
             nc.scalar.activation(
                 out=squares[:], in_=gate[ft][:], func=ACT.Square, bias=moments[ft][:, 1, 0:1],
                 accum_out=moments[ft][:, 1, 1:2],
@@ -236,8 +264,6 @@ def tile_lstmcell_kernel(
                 out=ratio[ft][:], in0=slope[ft][:, 0:1], scalar1=spread[ft][:, 1:2], scalar2=inv_std[ft][:, 1:2],
                 op0=ALU.mult, op1=ALU.mult,
             )
-
-        def shifts(ft):
             nc.gpsimd.tensor_scalar(
                 out=centre[ft][:], in0=moments[ft][:, 0, 0:1], scalar1=ratio[ft][:], scalar2=moments[ft][:, 1, 0:1],
                 op0=ALU.mult, op1=ALU.subtract,
@@ -252,10 +278,10 @@ def tile_lstmcell_kernel(
                 op0=ALU.mult, op1=ALU.add,
             )
 
-        def activate(ft):
+        def activate(ft, cols=slice(0, BATCH)):
             func = ACT.Tanh if ft // HALVES == CELL else ACT.Sigmoid
             nc.scalar.activation(
-                out=gate[ft][:], in_=gate[ft][:], func=func, scale=slope[ft][:, 1:2], bias=shift[ft][:]
+                out=gate[ft][:, cols], in_=gate[ft][:, cols], func=func, scale=slope[ft][:, 1:2], bias=shift[ft][:]
             )
 
         tanh_c = [keep.tile([P, BATCH], F32, name="tanh_c%d" % half) for half in range(HALVES)]
@@ -268,22 +294,32 @@ def tile_lstmcell_kernel(
         def tile_of(kind, half):
             return HALVES * kind + half
 
-        def keep_old(half):
+        def keep_old(half, j):
+            cT = bank([P, CHUNK], BF16, "v")
+            for i in range(TILES_PER_CHUNK):
+                nc.tensor.transpose(
+                    cT[:, i * P : (i + 1) * P], c_sb[:, j * TILES_PER_CHUNK + i, half * P : (half + 1) * P], ident_bf[:]
+                )
             forget = gate[tile_of(FORGET, half)]
-            nc.gpsimd.tensor_tensor(out=forget[:], in0=forget[:], in1=cT[:, half, :], op=ALU.mult)
+            nc.vector.tensor_tensor(out=forget[:, chunk(j)], in0=forget[:, chunk(j)], in1=cT[:], op=ALU.mult)
 
-        def take_new(half, engine):
+        def take_new(half, j, engine):
             in_gate = gate[tile_of(IN, half)]
-            engine.tensor_tensor(out=in_gate[:], in0=in_gate[:], in1=gate[tile_of(CELL, half)][:], op=ALU.mult)
+            engine.tensor_tensor(
+                out=in_gate[:, chunk(j)], in0=in_gate[:, chunk(j)], in1=gate[tile_of(CELL, half)][:, chunk(j)],
+                op=ALU.mult,
+            )
 
-        def sum_cell(half, engine):
+        def sum_cell(half, j, engine):
             raw = gate[tile_of(FORGET, half)]
-            engine.tensor_tensor(out=raw[:], in0=raw[:], in1=gate[tile_of(IN, half)][:], op=ALU.add)
+            engine.tensor_tensor(
+                out=raw[:, chunk(j)], in0=raw[:, chunk(j)], in1=gate[tile_of(IN, half)][:, chunk(j)], op=ALU.add
+            )
 
-        def measure_cell(half):
-            raw = gate[tile_of(FORGET, half)]
-            for j in range(N_CHUNKS):
-                nc.vector.bn_stats(out=c_stats[half][:, j, :], in_=raw[:, chunk(j)])
+        def measure_cell(half, j):
+            nc.vector.bn_stats(out=c_stats[half][:, j, :], in_=gate[tile_of(FORGET, half)][:, chunk(j)])
+
+        def cell_moments(half):
             nc.vector.bn_aggr(out=c_mean_var[half][:], in_=c_stats[half][:].rearrange("p j s -> p (j s)"))
 
         def cell_slope(half):
@@ -298,11 +334,18 @@ def tile_lstmcell_kernel(
                 out=c_shift[half][:], in0=offset_c[:, half : half + 1], in1=c_shift[half][:], op=ALU.subtract
             )
 
-        def norm_cell(half):
-            nc.gpsimd.tensor_scalar(
-                out=c_next[half][:], in0=gate[tile_of(FORGET, half)][:], scalar1=c_slope[half][:],
-                scalar2=c_shift[half][:], op0=ALU.mult, op1=ALU.add,
-            )
+        def norm_cell(half, j, engine):
+            raw = gate[tile_of(FORGET, half)]
+            if engine == nc.scalar:
+                nc.scalar.activation(
+                    out=c_next[half][:, chunk(j)], in_=raw[:, chunk(j)], func=ACT.Identity,
+                    scale=c_slope[half][:], bias=c_shift[half][:],
+                )
+            else:
+                engine.tensor_scalar(
+                    out=c_next[half][:, chunk(j)], in0=raw[:, chunk(j)], scalar1=c_slope[half][:],
+                    scalar2=c_shift[half][:], op0=ALU.mult, op1=ALU.add,
+                )
 
         def tanh_cell(half, j):
             nc.scalar.activation(
@@ -316,42 +359,78 @@ def tile_lstmcell_kernel(
                 out=h_next[:, chunk(j)], in0=h_next[:, chunk(j)], in1=tanh_c[half][:, chunk(j)], op=ALU.mult
             )
 
-        def flip(src, j, tag):
-            ps = bank([P, TILES_PER_CHUNK, P], F32, tag)
+        def store(src, j, dram, half, reader):
+            ps = bank([P, TILES_PER_CHUNK, P], F32, reader)
             for i in range(TILES_PER_CHUNK):
                 t = j * TILES_PER_CHUNK + i
                 nc.tensor.transpose(ps[:, i, :], src[:, t * P : (t + 1) * P], ident_f32[:])
-            return ps
-
-        def unload(ps, j, dram, half, i):
             rows = dram.rearrange("(p t) f -> p t f", t=ROW_TILES)
             tiles = slice(j * TILES_PER_CHUNK, (j + 1) * TILES_PER_CHUNK)
-            staged = keep.tile([P, TILES_PER_CHUNK, P], F32, name="staged", tag="staged", bufs=8)
-            copy_out(i, staged[:], ps[:])
+            staged = keep.tile([P, TILES_PER_CHUNK, P], F32, name="staged", tag="staged", bufs=16)
+            copy_out(reader, staged[:], ps[:])
             nc.sync.dma_start(out=rows[:, tiles, half * P : (half + 1) * P], in_=staged[:])
 
-        order = [tile_of(kind, half) for half in range(HALVES) for kind in (FORGET, IN, CELL)]
-        order += [tile_of(OUT, half) for half in range(HALVES)]
+        h_staged = {}
 
-        def first_tile_chunk(j):
+        def stage_hidden(half, j, reader):
+            if j not in h_staged:
+                h_staged[j] = keep.tile([P, TILES_PER_CHUNK, N_HID], F32, name="h_staged%d" % j)
+            ps = bank([P, TILES_PER_CHUNK, P], F32, reader)
+            for i in range(TILES_PER_CHUNK):
+                t = j * TILES_PER_CHUNK + i
+                nc.tensor.transpose(ps[:, i, :], gate[tile_of(OUT, half)][:, t * P : (t + 1) * P], ident_f32[:])
+            copy_out(reader, h_staged[j][:, :, half * P : (half + 1) * P], ps[:])
+
+        def store_hidden(j):
+            rows = out_1.rearrange("(p t) f -> p t f", t=ROW_TILES)
+            nc.sync.dma_start(out=rows[:, j * TILES_PER_CHUNK : (j + 1) * TILES_PER_CHUNK, :], in_=h_staged[j][:])
+
+        order = [tile_of(kind, half) for kind, half in ORDER]
+
+        for n in range(N_TILES):
+            for j in range(N_CHUNKS):
+                hh_reader[(order[n], j)] = "v" if (n >= 2 and j >= N_CHUNKS - HH_CHUNKS_ON_VECTOR) else "s"
+
+        def hidden_chunk(ft, j):
             for kt in range(K_TILES):
-                hidden_pass(order[0], K_TILES * j + kt)
-            hidden_out(order[0], j)
-            input_stats(order[0], j)
+                hidden_pass(ft, K_TILES * j + kt)
+            if hh_reader[(ft, j)] == "v":
+                hidden_out(ft, j)
 
+        def hidden_outs(ft):
+            for j in range(N_CHUNKS):
+                if hh_reader[(ft, j)] == "s":
+                    hidden_out(ft, j)
+            hidden_mean(ft)
+
+        transpose_x(0, "vs")
+        transpose_rows(whhT, whh_sb, 0, "vs")
+        transpose_rows(whhT, whh_sb, 1, "vs")
+        quantise_x(0)
         for j in range(N_CHUNKS):
-            transpose_rows(cT, c_sb, j)
-        for j in range(N_CHUNKS):
-            transpose_x(j)
-            if j == 0:
-                transpose_rows(whhT, whh_sb, 0)
-                transpose_rows(whhT, whh_sb, 1)
-            transpose_rows(hT, h_sb, j)
+            transpose_rows(hT, h_sb, j, "vs")
+            for n in (2 * j, 2 * j + 1):
+                input_stats(order[n], 0)
+            if j >= 1:
+                hidden_chunk(order[0], j - 1)
+                hidden_out(order[0], j - 1)
+        hidden_chunk(order[0], N_CHUNKS - 1)
+        hidden_out(order[0], N_CHUNKS - 1)
+        hidden_mean(order[0])
+        hidden_spread(order[0])
+        transpose_x(1, "vv")
+        for j in range(1, N_CHUNKS):
+            hidden_chunk(order[1], j - 1)
+            hidden_out(order[1], j - 1)
+            if j + 1 < N_CHUNKS:
+                transpose_x(j + 1, "vv")
             quantise_x(j)
-            if j > 0:
-                first_tile_chunk(j - 1)
+        hidden_chunk(order[1], N_CHUNKS - 1)
+        hidden_out(order[1], N_CHUNKS - 1)
+        hidden_mean(order[1])
+        hidden_spread(order[1])
 
-        par_ps = bank([P, P], BF16, "ih")
+        par_ps = bank([P, P], BF16, "v")
         nc.tensor.transpose(par_ps[:], par_rows[:], ident_bf[:])
         par = keep.tile([P, n_par], F32, name="par")
         nc.vector.tensor_copy(out=par[:], in_=par_ps[:, 0:n_par])
@@ -373,70 +452,53 @@ def tile_lstmcell_kernel(
         nc.vector.reciprocal(out=small[:], in_=by_vec[:, 1, :])
         nc.vector.tensor_tensor(out=by_vec[:, 0, :], in0=by_vec[:, 0, :], in1=small[:], op=ALU.mult)
 
-        first_tile_chunk(N_CHUNKS - 1)
-        hidden_moments(order[0])
-        input_moments(order[0])
-        for i in range(N_CHUNKS * K_TILES):
-            hidden_pass(order[1], i)
 
-        def kind_at(s):
-            return order[s] // HALVES if s >= 0 else None
+        def measure_input(n):
+            for j in range(1, N_CHUNKS):
+                input_stats(order[n], j)
+                if j < N_CHUNKS - 1 and n + 1 < N_TILES and n >= 1:
+                    hidden_chunk(order[n + 1], j + 1)
+            input_moments(order[n])
 
-        for s in range(1, N_TILES):
-            now, before = order[s], order[s - 1]
-            for j in range(N_CHUNKS):
-                hidden_out(now, j)
-            hidden_moments(now)
-            if s >= 2:
-                activate(order[s - 2])
-            slopes(before)
-            shifts(before)
-            if kind_at(s - 4) == FORGET:
-                keep_old(order[s - 4] % HALVES)
-            elif kind_at(s - 3) == CELL:
-                take_new(order[s - 3] % HALVES, nc.gpsimd)
-            elif kind_at(s - 4) == CELL:
-                sum_cell(order[s - 4] % HALVES, nc.gpsimd)
-            for j in range(N_CHUNKS):
-                input_stats(now, j)
-                if s + 1 < N_TILES:
-                    hidden_pass(order[s + 1], j)
-            input_moments(now)
-            for j in range(N_CHUNKS):
-                add_input(before, j)
-                if s + 1 < N_TILES:
-                    hidden_pass(order[s + 1], N_CHUNKS + j)
-            if kind_at(s - 5) == CELL:
-                measure_cell(order[s - 5] % HALVES)
+        def half_at(n):
+            return order[n] % HALVES
 
-        last = order[N_TILES - 1]
-        activate(order[N_TILES - 2])
-        slopes(last)
-        shifts(last)
-        cell_slope(0)
-        norm_cell(0)
-        take_new(1, nc.vector)
-        for j in range(N_CHUNKS):
-            add_input(last, j)
-        activate(last)
-        for j in range(N_CHUNKS):
-            tanh_cell(0, j)
-        sum_cell(1, nc.vector)
-        measure_cell(1)
-        cell_slope(1)
-        norm_cell(1)
-        for j in range(N_CHUNKS):
-            unload(flip(c_next[0], j, "hh"), j, out_0, 0, 1)
-        for j in range(N_CHUNKS):
-            gate_hidden(0, j, nc.vector)
-        flipped = [flip(gate[tile_of(OUT, 0)], j, "ih") for j in range(N_CHUNKS)]
-        for j in range(N_CHUNKS):
-            tanh_cell(1, j)
-        for j in range(N_CHUNKS):
-            unload(flipped[j], j, out_1, 0, 0)
-        for j in range(N_CHUNKS):
-            gate_hidden(1, j, nc.vector)
-        for j in range(N_CHUNKS):
-            unload(flip(gate[tile_of(OUT, 1)], j, "hh"), j, out_1, 1, j + 1)
-        for j in range(N_CHUNKS):
-            unload(flip(c_next[1], j, "ih"), j, out_0, 1, j + 1)
+        measure_input(0)
+        slopes(order[0])
+        hidden_chunk(order[2], 0)
+        hidden_chunk(order[2], 1)
+
+        def each_chunk(*stages):
+            for j in range(N_CHUNKS):
+                for stage in stages:
+                    stage(j)
+
+        plan = {}
+
+        def at(step, slot, work):
+            plan.setdefault((step, slot), []).append(work)
+
+        def run(step, slot):
+            for work in plan.get((step, slot), []):
+                work()
+
+        PLAN(at, each_chunk, order.index, tile_of, take_new, keep_old, sum_cell, measure_cell, cell_moments, cell_slope,
+             norm_cell, tanh_cell, gate_hidden, store, nc, gate, c_next, out_0, out_1, stage_hidden, store_hidden)
+
+        for n in range(N_TILES + 4):
+            if n + 1 < N_TILES:
+                measure_input(n + 1)
+                slopes(order[n + 1])
+            if n + 2 < N_TILES:
+                hidden_outs(order[n + 2])
+            if 1 <= n <= N_TILES:
+                activate(order[n - 1])
+            if n + 2 < N_TILES:
+                hidden_spread(order[n + 2])
+            run(n, "mid")
+            if n < N_TILES:
+                for j in range(N_CHUNKS):
+                    add_input(order[n], j)
+                    if j % 2 == 1 and n + 3 < N_TILES:
+                        hidden_chunk(order[n + 3], j // 2)
+            run(n, "end")

@@ -40,15 +40,19 @@ ORDER = [(IN, 0), (CELL, 0), (FORGET, 0), (IN, 1), (CELL, 1), (FORGET, 1), (OUT,
 
 def PLAN(at, each_chunk, pos, tile_of, take_new, keep_old, sum_cell, measure_cell, cell_moments, cell_slope,
          norm_cell, tanh_cell, gate_hidden, store, nc, gate, c_next, out_0, out_1, stage_hidden, store_hidden):
-    at(2, "mid", lambda: each_chunk(lambda j: take_new(0, j, nc.gpsimd)))
+    at(2, "end", lambda: each_chunk(lambda j: take_new(0, j, nc.gpsimd)))
     at(4, "mid", lambda: each_chunk(lambda j: keep_old(0, j), lambda j: sum_cell(0, j, nc.gpsimd)))
     at(5, "mid", lambda: (each_chunk(lambda j: measure_cell(0, j)), cell_moments(0), cell_slope(0)))
-    at(5, "end", lambda: each_chunk(lambda j: take_new(1, j, nc.gpsimd)))
-    at(6, "end", lambda: each_chunk(lambda j: keep_old(1, j), lambda j: sum_cell(1, j, nc.gpsimd)))
+    at(5, "end", lambda: (take_new(1, 0, nc.gpsimd), take_new(1, 1, nc.gpsimd)))
+    at(6, "end", lambda: (take_new(1, 2, nc.gpsimd), take_new(1, 3, nc.gpsimd)))
+    at(6, "end", lambda: (keep_old(1, 0), keep_old(1, 1), sum_cell(1, 0, nc.vector), keep_old(1, 2), sum_cell(1, 1, nc.vector),
+                          measure_cell(1, 0), keep_old(1, 3), sum_cell(1, 2, nc.vector), measure_cell(1, 1), sum_cell(1, 3, nc.vector),
+                          measure_cell(1, 2)))
+    at(7, "mid", lambda: (measure_cell(1, 3),))
+    at(6, "end", lambda: each_chunk(lambda j: norm_cell(0, j, nc.scalar)))
+    at(6, "end", lambda: each_chunk(lambda j: store(c_next[0], j, out_0, 0, "s")))
     at(7, "mid", lambda: each_chunk(lambda j: tanh_cell(0, j)))
-    at(7, "mid", lambda: each_chunk(lambda j: norm_cell(0, j, nc.scalar)))
-    at(7, "end", lambda: (each_chunk(lambda j: measure_cell(1, j)), cell_moments(1), cell_slope(1)))
-    at(7, "end", lambda: each_chunk(lambda j: store(c_next[0], j, out_0, 0, "s")))
+    at(7, "end", lambda: (cell_moments(1), cell_slope(1)))
     at(8, "mid", lambda: each_chunk(lambda j: gate_hidden(0, j, nc.vector)))
     at(8, "mid", lambda: each_chunk(lambda j: tanh_cell(1, j)))
     at(8, "mid", lambda: each_chunk(lambda j: norm_cell(1, j, nc.vector)))
@@ -88,6 +92,8 @@ def tile_lstmcell_kernel(
         make_identity(nc, ident_f32[:])
         minus_half = keep.tile([P, 2], F32, name="minus_half")
         nc.vector.memset(minus_half[:], -0.5)
+        minus_one = keep.tile([P, N_TILES], F32, name="minus_one")
+        nc.vector.memset(minus_one[:], -1.0)
         eps2 = keep.tile([P, 2], F32, name="eps2")
         nc.vector.memset(eps2[:, 0:1], EPS)
         nc.vector.memset(eps2[:, 1:2], BATCH * EPS)
@@ -125,14 +131,14 @@ def tile_lstmcell_kernel(
             load_chunk(whh_sb, whh_rows, j)
         for j in range(N_CHUNKS):
             load_chunk(h_sb, h_rows, j)
-        for j in range(1, N_CHUNKS):
-            load_chunk(x_sb, x_rows, j)
         row = 0
         for vec in (g_ih, g_hh, b, b_ih, b_hh, g_c, b_c):
             n_rows = vec.shape[0] // P
             nc.sync.dma_start(out=par_rows[row : row + n_rows, :], in_=vec.rearrange("(a j) -> a j", j=P))
             row += n_rows
         n_par = row
+        for j in range(1, N_CHUNKS):
+            load_chunk(x_sb, x_rows, j)
         for j in range(N_CHUNKS):
             load_chunk(c_sb, c_rows, j)
 
@@ -256,20 +262,38 @@ def tile_lstmcell_kernel(
             nc.gpsimd.tensor_tensor(out=out, in0=variances, in1=eps2[:, 0:width], op=ALU.add)
             nc.gpsimd.tensor_tensor(out=out, in0=out, in1=minus_half[:, 0:width], op=ALU.pow)
 
-        def slopes(ft):
-            nc.gpsimd.tensor_tensor(out=spread[ft][:], in0=moments[ft][:, :, 1], in1=eps2[:], op=ALU.add)
-            nc.gpsimd.tensor_tensor(out=inv_std[ft][:], in0=spread[ft][:], in1=minus_half[:], op=ALU.pow)
-            nc.gpsimd.tensor_tensor(out=slope[ft][:], in0=inv_std[ft][:], in1=by_vec[:, 0:2, ft], op=ALU.mult)
-            nc.gpsimd.tensor_scalar(
-                out=ratio[ft][:], in0=slope[ft][:, 0:1], scalar1=spread[ft][:, 1:2], scalar2=inv_std[ft][:, 1:2],
-                op0=ALU.mult, op1=ALU.mult,
-            )
-            nc.gpsimd.tensor_scalar(
-                out=centre[ft][:], in0=moments[ft][:, 0, 0:1], scalar1=ratio[ft][:], scalar2=moments[ft][:, 1, 0:1],
-                op0=ALU.mult, op1=ALU.subtract,
-            )
-            nc.gpsimd.tensor_tensor(out=centre[ft][:], in0=centre[ft][:], in1=slope[ft][:, 1:2], op=ALU.mult)
-            nc.gpsimd.tensor_tensor(out=shift[ft][:], in0=offsets[:, ft : ft + 1], in1=centre[ft][:], op=ALU.subtract)
+        def ratio_steps(ft):
+            return [
+                lambda: nc.gpsimd.tensor_tensor(out=spread[ft][:], in0=moments[ft][:, :, 1], in1=eps2[:], op=ALU.add),
+                lambda: nc.gpsimd.tensor_tensor(out=inv_std[ft][:], in0=spread[ft][:], in1=minus_half[:], op=ALU.pow),
+                lambda: nc.gpsimd.tensor_tensor(
+                    out=slope[ft][:], in0=inv_std[ft][:], in1=by_vec[:, 0:2, ft], op=ALU.mult
+                ),
+                lambda: nc.gpsimd.tensor_scalar(
+                    out=ratio[ft][:], in0=slope[ft][:, 0:1], scalar1=spread[ft][:, 1:2],
+                    scalar2=inv_std[ft][:, 1:2], op0=ALU.mult, op1=ALU.mult,
+                ),
+            ]
+
+        def shift_steps(ft):
+            return [
+                lambda: nc.gpsimd.tensor_scalar(
+                    out=centre[ft][:], in0=moments[ft][:, 0, 0:1], scalar1=ratio[ft][:],
+                    scalar2=moments[ft][:, 1, 0:1], op0=ALU.mult, op1=ALU.subtract,
+                ),
+                lambda: nc.gpsimd.tensor_tensor(
+                    out=centre[ft][:], in0=centre[ft][:], in1=slope[ft][:, 1:2], op=ALU.mult
+                ),
+                lambda: nc.gpsimd.tensor_tensor(
+                    out=shift[ft][:], in0=offsets[:, ft : ft + 1], in1=centre[ft][:], op=ALU.subtract
+                ),
+            ]
+
+        def weave(first, second):
+            for i in range(max(len(first), len(second))):
+                for steps in (first, second):
+                    if i < len(steps):
+                        steps[i]()
 
         def add_input(ft, j):
             ih = input_product(ft, j)
@@ -401,7 +425,6 @@ def tile_lstmcell_kernel(
             for j in range(N_CHUNKS):
                 if hh_reader[(ft, j)] == "s":
                     hidden_out(ft, j)
-            hidden_mean(ft)
 
         transpose_x(0, "vs")
         transpose_rows(whhT, whh_sb, 0, "vs")
@@ -418,6 +441,30 @@ def tile_lstmcell_kernel(
         hidden_out(order[0], N_CHUNKS - 1)
         hidden_mean(order[0])
         hidden_spread(order[0])
+        par_ps = bank([P, P], BF16, "v")
+        nc.tensor.transpose(par_ps[:], par_rows[:], ident_bf[:])
+        par = keep.tile([P, n_par], F32, name="par")
+        nc.vector.tensor_copy(out=par[:], in_=par_ps[:, 0:n_par])
+        by_vec = par[:, 0 : 5 * N_TILES].rearrange("p (v a) -> p v a", a=N_TILES)
+        gain_c = par[:, 5 * N_TILES : 5 * N_TILES + HALVES]
+        offset_c = par[:, 5 * N_TILES + HALVES : 5 * N_TILES + 2 * HALVES]
+        offsets = keep.tile([P, N_TILES], F32, name="offsets")
+        nc.gpsimd.tensor_tensor(out=offsets[:], in0=by_vec[:, 2, :], in1=by_vec[:, 3, :], op=ALU.add)
+        small = keep.tile([P, N_TILES], F32, name="small")
+        nc.gpsimd.tensor_tensor(out=small[:], in0=by_vec[:, 1, :], in1=by_vec[:, 1, :], op=ALU.mult)
+        nc.gpsimd.tensor_tensor(out=offsets[:], in0=offsets[:], in1=by_vec[:, 4, :], op=ALU.add)
+        nc.gpsimd.tensor_scalar(
+            out=small[:], in0=small[:], scalar1=TINY_GAIN * TINY_GAIN, scalar2=TINY_GAIN, op0=ALU.is_lt, op1=ALU.mult
+        )
+        nc.gpsimd.tensor_tensor(out=small[:], in0=by_vec[:, 1, :], in1=small[:], op=ALU.add)
+        nc.gpsimd.tensor_scalar(
+            out=by_vec[:, 1, :], in0=small[:], scalar1=math.sqrt(BATCH), scalar2=0.0, op0=ALU.mult, op1=ALU.add
+        )
+        nc.gpsimd.tensor_tensor(out=small[:], in0=by_vec[:, 1, :], in1=by_vec[:, 1, :], op=ALU.mult)
+        nc.gpsimd.tensor_tensor(out=small[:], in0=small[:], in1=minus_one[:], op=ALU.pow)
+        nc.gpsimd.tensor_tensor(out=small[:], in0=small[:], in1=by_vec[:, 1, :], op=ALU.mult)
+        nc.gpsimd.tensor_tensor(out=by_vec[:, 0, :], in0=by_vec[:, 0, :], in1=small[:], op=ALU.mult)
+
         transpose_x(1, "vv")
         for j in range(1, N_CHUNKS):
             hidden_chunk(order[1], j - 1)
@@ -430,41 +477,18 @@ def tile_lstmcell_kernel(
         hidden_mean(order[1])
         hidden_spread(order[1])
 
-        par_ps = bank([P, P], BF16, "v")
-        nc.tensor.transpose(par_ps[:], par_rows[:], ident_bf[:])
-        par = keep.tile([P, n_par], F32, name="par")
-        nc.vector.tensor_copy(out=par[:], in_=par_ps[:, 0:n_par])
-        by_vec = par[:, 0 : 5 * N_TILES].rearrange("p (v a) -> p v a", a=N_TILES)
-        gain_c = par[:, 5 * N_TILES : 5 * N_TILES + HALVES]
-        offset_c = par[:, 5 * N_TILES + HALVES : 5 * N_TILES + 2 * HALVES]
-        offsets = keep.tile([P, N_TILES], F32, name="offsets")
-        nc.vector.tensor_add(out=offsets[:], in0=by_vec[:, 2, :], in1=by_vec[:, 3, :])
-        nc.vector.tensor_add(out=offsets[:], in0=offsets[:], in1=by_vec[:, 4, :])
-        small = keep.tile([P, N_TILES], F32, name="small")
-        nc.vector.tensor_tensor(out=small[:], in0=by_vec[:, 1, :], in1=by_vec[:, 1, :], op=ALU.mult)
-        nc.vector.tensor_scalar(
-            out=small[:], in0=small[:], scalar1=TINY_GAIN * TINY_GAIN, scalar2=TINY_GAIN, op0=ALU.is_lt, op1=ALU.mult
-        )
-        nc.vector.tensor_tensor(out=by_vec[:, 1, :], in0=by_vec[:, 1, :], in1=small[:], op=ALU.add)
-        nc.vector.tensor_scalar(
-            out=by_vec[:, 1, :], in0=by_vec[:, 1, :], scalar1=math.sqrt(BATCH), scalar2=None, op0=ALU.mult
-        )
-        nc.vector.reciprocal(out=small[:], in_=by_vec[:, 1, :])
-        nc.vector.tensor_tensor(out=by_vec[:, 0, :], in0=by_vec[:, 0, :], in1=small[:], op=ALU.mult)
-
-
         def measure_input(n):
             for j in range(1, N_CHUNKS):
                 input_stats(order[n], j)
                 if j < N_CHUNKS - 1 and n + 1 < N_TILES and n >= 1:
                     hidden_chunk(order[n + 1], j + 1)
-            input_moments(order[n])
 
         def half_at(n):
             return order[n] % HALVES
 
         measure_input(0)
-        slopes(order[0])
+        input_moments(order[0])
+        weave(ratio_steps(order[0]), [])
         hidden_chunk(order[2], 0)
         hidden_chunk(order[2], 1)
 
@@ -488,17 +512,24 @@ def tile_lstmcell_kernel(
         for n in range(N_TILES + 4):
             if n + 1 < N_TILES:
                 measure_input(n + 1)
-                slopes(order[n + 1])
             if n + 2 < N_TILES:
                 hidden_outs(order[n + 2])
             if 1 <= n <= N_TILES:
-                activate(order[n - 1])
+                activate(order[n - 1], slice(0, BATCH // 2))
+            if n + 2 < N_TILES:
+                hidden_mean(order[n + 2])
+            if 1 <= n <= N_TILES:
+                activate(order[n - 1], slice(BATCH // 2, BATCH))
             if n + 2 < N_TILES:
                 hidden_spread(order[n + 2])
             run(n, "mid")
             if n < N_TILES:
                 for j in range(N_CHUNKS):
                     add_input(order[n], j)
+                    if j == 0:
+                        if n + 1 < N_TILES:
+                            input_moments(order[n + 1])
+                        weave(ratio_steps(order[n + 1]) if n + 1 < N_TILES else [], shift_steps(order[n]))
                     if j % 2 == 1 and n + 3 < N_TILES:
                         hidden_chunk(order[n + 3], j // 2)
             run(n, "end")

@@ -39,7 +39,7 @@ ORDER = [(IN, 0), (CELL, 0), (FORGET, 0), (IN, 1), (CELL, 1), (FORGET, 1), (OUT,
 
 
 def PLAN(at, each_chunk, pos, tile_of, take_new, keep_old, sum_cell, measure_cell, cell_moments, cell_slope,
-         norm_cell, tanh_cell, gate_hidden, store, nc, gate, c_next, out_0, out_1, stage_hidden, store_hidden):
+         norm_cell, tanh_cell, gate_hidden, store, nc, gate, c_next, out_0, out_1, stage_hidden, store_hidden, norm_whole_cell):
     at(2, "end", lambda: each_chunk(lambda j: take_new(0, j, nc.gpsimd)))
     at(4, "mid", lambda: each_chunk(lambda j: keep_old(0, j), lambda j: sum_cell(0, j, nc.gpsimd)))
     at(5, "mid", lambda: (each_chunk(lambda j: measure_cell(0, j)), cell_moments(0), cell_slope(0)))
@@ -47,12 +47,11 @@ def PLAN(at, each_chunk, pos, tile_of, take_new, keep_old, sum_cell, measure_cel
     at(6, "end", lambda: (take_new(1, 2, nc.gpsimd), take_new(1, 3, nc.gpsimd)))
     at(6, "end", lambda: (keep_old(1, 0), keep_old(1, 1), sum_cell(1, 0, nc.vector), keep_old(1, 2), sum_cell(1, 1, nc.vector),
                           measure_cell(1, 0), keep_old(1, 3), sum_cell(1, 2, nc.vector), measure_cell(1, 1), sum_cell(1, 3, nc.vector),
-                          measure_cell(1, 2)))
-    at(7, "mid", lambda: (measure_cell(1, 3),))
-    at(6, "end", lambda: each_chunk(lambda j: norm_cell(0, j, nc.scalar)))
+                          measure_cell(1, 2), measure_cell(1, 3)))
+    at(6, "mid", lambda: norm_whole_cell(0))
     at(6, "end", lambda: each_chunk(lambda j: store(c_next[0], j, out_0, 0, "s")))
     at(7, "mid", lambda: each_chunk(lambda j: tanh_cell(0, j)))
-    at(7, "end", lambda: (cell_moments(1), cell_slope(1)))
+    at(7, "first", lambda: (cell_moments(1), cell_slope(1)))
     at(8, "mid", lambda: each_chunk(lambda j: gate_hidden(0, j, nc.vector)))
     at(8, "mid", lambda: each_chunk(lambda j: tanh_cell(1, j)))
     at(8, "mid", lambda: each_chunk(lambda j: norm_cell(1, j, nc.vector)))
@@ -120,6 +119,8 @@ def tile_lstmcell_kernel(
         nc.vector.memset(w_plane[:].bitcast(I32), 0)
 
         w_words = keep.tile([P, 2 * N_GATES], U8, name="w_words", align_bytes=64)
+        load_chunk(whh_sb, whh_rows, 0)
+        load_chunk(h_sb, h_rows, 0)
         load_chunk(x_sb, x_rows, 0)
         nc.sync.dma_start(out=w_words[:].bitcast(I32), in_=w_ih_words[0].bitcast(I32))
         for quad in range(4):
@@ -127,9 +128,9 @@ def tile_lstmcell_kernel(
                 out=w_plane[32 * quad : 32 * quad + 4, :].bitcast(I32),
                 in_=w_ih_scales[0, 4 * quad : 4 * quad + 4, :].bitcast(I32),
             )
-        for j in range(2):
-            load_chunk(whh_sb, whh_rows, j)
-        for j in range(N_CHUNKS):
+        load_chunk(h_sb, h_rows, 1)
+        load_chunk(whh_sb, whh_rows, 1)
+        for j in range(2, N_CHUNKS):
             load_chunk(h_sb, h_rows, j)
         row = 0
         for vec in (g_ih, g_hh, b, b_ih, b_hh, g_c, b_c):
@@ -371,6 +372,12 @@ def tile_lstmcell_kernel(
                     scalar2=c_shift[half][:], op0=ALU.mult, op1=ALU.add,
                 )
 
+        def norm_whole_cell(half):
+            nc.vector.tensor_scalar(
+                out=c_next[half][:], in0=gate[tile_of(FORGET, half)][:], scalar1=c_slope[half][:],
+                scalar2=c_shift[half][:], op0=ALU.mult, op1=ALU.add,
+            )
+
         def tanh_cell(half, j):
             nc.scalar.activation(
                 out=tanh_c[half][:, chunk(j)], in_=gate[tile_of(FORGET, half)][:, chunk(j)], func=ACT.Tanh,
@@ -423,23 +430,36 @@ def tile_lstmcell_kernel(
 
         def hidden_outs(ft):
             for j in range(N_CHUNKS):
-                if hh_reader[(ft, j)] == "s":
+                if hh_reader[(ft, j)] == "s" and not (ft == order[2] and j < 2):
                     hidden_out(ft, j)
 
-        transpose_x(0, "vs")
-        transpose_rows(whhT, whh_sb, 0, "vs")
-        transpose_rows(whhT, whh_sb, 1, "vs")
-        quantise_x(0)
-        for j in range(N_CHUNKS):
-            transpose_rows(hT, h_sb, j, "vs")
-            for n in (2 * j, 2 * j + 1):
+        def first_stats(pair):
+            for n in (2 * pair, 2 * pair + 1):
                 input_stats(order[n], 0)
-            if j >= 1:
-                hidden_chunk(order[0], j - 1)
-                hidden_out(order[0], j - 1)
-        hidden_chunk(order[0], N_CHUNKS - 1)
-        hidden_out(order[0], N_CHUNKS - 1)
+
+        def whole_chunk(n, j):
+            hidden_chunk(order[n], j)
+            hidden_out(order[n], j)
+
+        transpose_rows(whhT, whh_sb, 0, "vs")
+        transpose_rows(hT, h_sb, 0, "vs")
+        transpose_x(0, "vs")
+        whole_chunk(0, 0)
+        quantise_x(0)
+        transpose_rows(hT, h_sb, 1, "vs")
+        first_stats(0)
+        whole_chunk(0, 1)
+        transpose_rows(whhT, whh_sb, 1, "vs")
+        first_stats(1)
+        transpose_rows(hT, h_sb, 2, "vs")
+        first_stats(2)
+        whole_chunk(0, 2)
+        transpose_rows(hT, h_sb, 3, "vs")
+        first_stats(3)
+        whole_chunk(0, 3)
+        whole_chunk(1, 0)
         hidden_mean(order[0])
+        whole_chunk(1, 1)
         hidden_spread(order[0])
         par_ps = bank([P, P], BF16, "v")
         nc.tensor.transpose(par_ps[:], par_rows[:], ident_bf[:])
@@ -466,16 +486,19 @@ def tile_lstmcell_kernel(
         nc.gpsimd.tensor_tensor(out=by_vec[:, 0, :], in0=by_vec[:, 0, :], in1=small[:], op=ALU.mult)
 
         transpose_x(1, "vv")
-        for j in range(1, N_CHUNKS):
-            hidden_chunk(order[1], j - 1)
-            hidden_out(order[1], j - 1)
-            if j + 1 < N_CHUNKS:
-                transpose_x(j + 1, "vv")
-            quantise_x(j)
-        hidden_chunk(order[1], N_CHUNKS - 1)
-        hidden_out(order[1], N_CHUNKS - 1)
+        transpose_x(2, "vv")
+        quantise_x(1)
+        whole_chunk(1, 2)
+        transpose_x(3, "vv")
+        quantise_x(2)
+        whole_chunk(1, 3)
+        hidden_chunk(order[2], 0)
+        hidden_out(order[2], 0)
         hidden_mean(order[1])
+        hidden_chunk(order[2], 1)
+        hidden_out(order[2], 1)
         hidden_spread(order[1])
+        quantise_x(3)
 
         def measure_input(n):
             for j in range(1, N_CHUNKS):
@@ -489,8 +512,6 @@ def tile_lstmcell_kernel(
         measure_input(0)
         input_moments(order[0])
         weave(ratio_steps(order[0]), [])
-        hidden_chunk(order[2], 0)
-        hidden_chunk(order[2], 1)
 
         def each_chunk(*stages):
             for j in range(N_CHUNKS):
@@ -507,7 +528,7 @@ def tile_lstmcell_kernel(
                 work()
 
         PLAN(at, each_chunk, order.index, tile_of, take_new, keep_old, sum_cell, measure_cell, cell_moments, cell_slope,
-             norm_cell, tanh_cell, gate_hidden, store, nc, gate, c_next, out_0, out_1, stage_hidden, store_hidden)
+             norm_cell, tanh_cell, gate_hidden, store, nc, gate, c_next, out_0, out_1, stage_hidden, store_hidden, norm_whole_cell)
 
         for n in range(N_TILES + 4):
             if n + 1 < N_TILES:
@@ -530,6 +551,7 @@ def tile_lstmcell_kernel(
                         if n + 1 < N_TILES:
                             input_moments(order[n + 1])
                         weave(ratio_steps(order[n + 1]) if n + 1 < N_TILES else [], shift_steps(order[n]))
+                        run(n, "first")
                     if j % 2 == 1 and n + 3 < N_TILES:
                         hidden_chunk(order[n + 3], j // 2)
             run(n, "end")

@@ -35,6 +35,8 @@ BANKS = {"v": 4, "s": 4}
 
 HH_CHUNKS_ON_VECTOR = 1
 
+WARM_UP_PASSES = 5
+
 ORDER = [(IN, 0), (CELL, 0), (FORGET, 0), (IN, 1), (CELL, 1), (FORGET, 1), (OUT, 0), (OUT, 1)]
 
 
@@ -84,6 +86,12 @@ def tile_lstmcell_kernel(
                 nc.vector.tensor_copy(out=out, in_=in_)
             else:
                 nc.scalar.copy(out=out, in_=in_)
+
+        idle_work = keep.tile([P, CHUNK], BF16, name="idle_work")
+        nc.vector.memset(idle_work[:], 0.0)
+        for i in range(WARM_UP_PASSES):
+            unread = bank([P, CHUNK], F32, "vs"[i % 2])
+            nc.tensor.matmul(out=unread[:], lhsT=idle_work[:, 0:P], rhs=idle_work[:], start=True, stop=True)
 
         ident_bf = keep.tile([P, P], BF16, name="ident_bf")
         make_identity(nc, ident_bf[:])
@@ -447,15 +455,15 @@ def tile_lstmcell_kernel(
         whole_chunk(0, 0)
         quantise_x(0)
         transpose_rows(hT, h_sb, 1, "vs")
-        first_stats(0)
-        whole_chunk(0, 1)
         transpose_rows(whhT, whh_sb, 1, "vs")
+        first_stats(0)
         first_stats(1)
+        whole_chunk(0, 1)
         transpose_rows(hT, h_sb, 2, "vs")
-        first_stats(2)
-        whole_chunk(0, 2)
         transpose_rows(hT, h_sb, 3, "vs")
+        first_stats(2)
         first_stats(3)
+        whole_chunk(0, 2)
         whole_chunk(0, 3)
         whole_chunk(1, 0)
         hidden_mean(order[0])

@@ -54,13 +54,13 @@ def PLAN(at, each_chunk, pos, tile_of, take_new, keep_old, sum_cell, measure_cel
     at(6, "end", lambda: each_chunk(lambda j: store(c_next[0], j, out_0, 0, "s")))
     at(7, "mid", lambda: each_chunk(lambda j: tanh_cell(0, j)))
     at(7, "first", lambda: (cell_moments(1), cell_slope(1)))
-    at(8, "mid", lambda: each_chunk(lambda j: gate_hidden(0, j, nc.vector)))
-    at(8, "mid", lambda: each_chunk(lambda j: tanh_cell(1, j)))
     at(8, "mid", lambda: each_chunk(lambda j: norm_cell(1, j, nc.vector)))
+    at(8, "mid", lambda: each_chunk(lambda j: tanh_cell(1, j)))
+    at(8, "mid", lambda: each_chunk(lambda j: gate_hidden(0, j, nc.vector)))
+    at(8, "mid", lambda: each_chunk(lambda j: store(c_next[1], j, out_0, 1, "s")))
     at(8, "mid", lambda: each_chunk(lambda j: gate_hidden(1, j, nc.vector)))
-    at(8, "mid", lambda: each_chunk(lambda j: store(gate[tile_of(OUT, 0)], j, out_1, 0, "s")))
-    at(8, "mid", lambda: each_chunk(lambda j: store(c_next[1], j, out_0, 1, "v")))
-    at(8, "mid", lambda: each_chunk(lambda j: store(gate[tile_of(OUT, 1)], j, out_1, 1, "svsv"[j])))
+    at(8, "mid", lambda: each_chunk(lambda j: stage_hidden(0, j, "s")))
+    at(8, "mid", lambda: each_chunk(lambda j: stage_hidden(1, j, "v"), store_hidden))
 
 
 FLOPS = 2 * BATCH * N_GATES * (N_IN + N_HID)
@@ -405,7 +405,7 @@ def tile_lstmcell_kernel(
                 nc.tensor.transpose(ps[:, i, :], src[:, t * P : (t + 1) * P], ident_f32[:])
             rows = dram.rearrange("(p t) f -> p t f", t=ROW_TILES)
             tiles = slice(j * TILES_PER_CHUNK, (j + 1) * TILES_PER_CHUNK)
-            staged = keep.tile([P, TILES_PER_CHUNK, P], F32, name="staged", tag="staged", bufs=16)
+            staged = keep.tile([P, TILES_PER_CHUNK, P], F32, name="staged", tag="staged", bufs=8)
             copy_out(reader, staged[:], ps[:])
             nc.sync.dma_start(out=rows[:, tiles, half * P : (half + 1) * P], in_=staged[:])
 

@@ -46,21 +46,20 @@ def PLAN(at, each_chunk, pos, tile_of, take_new, keep_old, sum_cell, measure_cel
     at(4, "mid", lambda: each_chunk(lambda j: keep_old(0, j), lambda j: sum_cell(0, j, nc.gpsimd)))
     at(5, "mid", lambda: (each_chunk(lambda j: measure_cell(0, j)), cell_moments(0), cell_slope(0)))
     at(5, "end", lambda: (take_new(1, 0, nc.gpsimd), take_new(1, 1, nc.gpsimd)))
-    at(6, "end", lambda: (take_new(1, 2, nc.gpsimd), take_new(1, 3, nc.gpsimd)))
-    at(6, "end", lambda: (keep_old(1, 0), keep_old(1, 1), sum_cell(1, 0, nc.vector), keep_old(1, 2), sum_cell(1, 1, nc.vector),
-                          measure_cell(1, 0), keep_old(1, 3), sum_cell(1, 2, nc.vector), measure_cell(1, 1), sum_cell(1, 3, nc.vector),
-                          measure_cell(1, 2), measure_cell(1, 3)))
+    at(6, "end", lambda: (keep_old(1, 0), keep_old(1, 1), sum_cell(1, 0, nc.vector), take_new(1, 2, nc.vector), sum_cell(1, 1, nc.vector),
+                          keep_old(1, 2), measure_cell(1, 0), take_new(1, 3, nc.vector), measure_cell(1, 1), keep_old(1, 3),
+                          sum_cell(1, 2, nc.vector), sum_cell(1, 3, nc.vector), measure_cell(1, 2), measure_cell(1, 3)))
     at(6, "mid", lambda: norm_whole_cell(0))
     at(6, "end", lambda: each_chunk(lambda j: store(c_next[0], j, out_0, 0, "s")))
     at(7, "mid", lambda: each_chunk(lambda j: tanh_cell(0, j)))
     at(7, "first", lambda: (cell_moments(1), cell_slope(1)))
     at(8, "mid", lambda: each_chunk(lambda j: norm_cell(1, j, nc.vector)))
-    at(8, "mid", lambda: each_chunk(lambda j: tanh_cell(1, j)))
-    at(8, "mid", lambda: each_chunk(lambda j: gate_hidden(0, j, nc.vector)))
-    at(8, "mid", lambda: each_chunk(lambda j: store(c_next[1], j, out_0, 1, "s")))
-    at(8, "mid", lambda: each_chunk(lambda j: gate_hidden(1, j, nc.vector)))
-    at(8, "mid", lambda: each_chunk(lambda j: stage_hidden(0, j, "s")))
-    at(8, "mid", lambda: each_chunk(lambda j: stage_hidden(1, j, "v"), store_hidden))
+    at(8, "mid", lambda: each_chunk(lambda j: tanh_cell(1, j), lambda j: store(c_next[1], j, out_0, 1, "s")))
+    at(8, "mid", lambda: (gate_hidden(0, 0, nc.vector), gate_hidden(0, 1, nc.vector), gate_hidden(1, 0, nc.vector), gate_hidden(1, 1, nc.vector),
+                          stage_hidden(0, 0, "s"), stage_hidden(0, 1, "s"),
+                          gate_hidden(0, 2, nc.vector), gate_hidden(0, 3, nc.vector), stage_hidden(1, 0, "v"), store_hidden(0),
+                          gate_hidden(1, 2, nc.vector), stage_hidden(1, 1, "v"), store_hidden(1), gate_hidden(1, 3, nc.vector),
+                          stage_hidden(0, 2, "s"), stage_hidden(0, 3, "s"), stage_hidden(1, 2, "v"), store_hidden(2), stage_hidden(1, 3, "v"), store_hidden(3)))
 
 
 FLOPS = 2 * BATCH * N_GATES * (N_IN + N_HID)

@@ -44,22 +44,6 @@ def PLAN(at, each_chunk, pos, tile_of, take_new, keep_old, sum_cell, measure_cel
          norm_cell, tanh_cell, gate_hidden, store, nc, gate, c_next, out_0, out_1, stage_hidden, store_hidden, norm_whole_cell):
     at(2, "end", lambda: each_chunk(lambda j: take_new(0, j, nc.gpsimd)))
     at(4, "mid", lambda: each_chunk(lambda j: keep_old(0, j), lambda j: sum_cell(0, j, nc.gpsimd)))
-    at(5, "mid", lambda: (each_chunk(lambda j: measure_cell(0, j)), cell_moments(0), cell_slope(0)))
-    at(5, "end", lambda: (take_new(1, 0, nc.gpsimd), take_new(1, 1, nc.gpsimd)))
-    at(6, "end", lambda: (keep_old(1, 0), keep_old(1, 1), sum_cell(1, 0, nc.vector), take_new(1, 2, nc.vector), sum_cell(1, 1, nc.vector),
-                          keep_old(1, 2), measure_cell(1, 0), take_new(1, 3, nc.vector), measure_cell(1, 1), keep_old(1, 3),
-                          sum_cell(1, 2, nc.vector), sum_cell(1, 3, nc.vector), measure_cell(1, 2), measure_cell(1, 3)))
-    at(6, "mid", lambda: norm_whole_cell(0))
-    at(6, "end", lambda: each_chunk(lambda j: store(c_next[0], j, out_0, 0, "s")))
-    at(7, "mid", lambda: each_chunk(lambda j: tanh_cell(0, j)))
-    at(7, "first", lambda: (cell_moments(1), cell_slope(1)))
-    at(8, "mid", lambda: each_chunk(lambda j: norm_cell(1, j, nc.vector)))
-    at(8, "mid", lambda: each_chunk(lambda j: tanh_cell(1, j), lambda j: store(c_next[1], j, out_0, 1, "s")))
-    at(8, "mid", lambda: (gate_hidden(0, 0, nc.vector), gate_hidden(0, 1, nc.vector), gate_hidden(1, 0, nc.vector), gate_hidden(1, 1, nc.vector),
-                          stage_hidden(0, 0, "s"), stage_hidden(0, 1, "s"),
-                          gate_hidden(0, 2, nc.vector), gate_hidden(0, 3, nc.vector), stage_hidden(1, 0, "v"), store_hidden(0),
-                          gate_hidden(1, 2, nc.vector), stage_hidden(1, 1, "v"), store_hidden(1), gate_hidden(1, 3, nc.vector),
-                          stage_hidden(0, 2, "s"), stage_hidden(0, 3, "s"), stage_hidden(1, 2, "v"), store_hidden(2), stage_hidden(1, 3, "v"), store_hidden(3)))
 
 
 FLOPS = 2 * BATCH * N_GATES * (N_IN + N_HID)
@@ -320,7 +304,10 @@ def tile_lstmcell_kernel(
         c_next = [keep.tile([P, BATCH], F32, name="c_next%d" % half) for half in range(HALVES)]
         c_stats = [keep.tile([P, N_CHUNKS, 6], F32, name="c_stats%d" % half) for half in range(HALVES)]
         c_mean_var = [keep.tile([P, 2], F32, name="c_mean_var%d" % half) for half in range(HALVES)]
-        c_slope = [keep.tile([P, 1], F32, name="c_slope%d" % half) for half in range(HALVES)]
+        c_inv = [keep.tile([P, 1], F32, name="c_inv%d" % half) for half in range(HALVES)]
+        c_pair = [keep.tile([P, 2], F32, name="c_pair%d" % half) for half in range(HALVES)]
+        c_slope = [c_pair[half][:, 0:1] for half in range(HALVES)]
+        gain_pairs = keep.tile([P, HALVES, 2], F32, name="gain_pairs")
         c_shift = [keep.tile([P, 1], F32, name="c_shift%d" % half) for half in range(HALVES)]
 
         def tile_of(kind, half):
@@ -354,16 +341,21 @@ def tile_lstmcell_kernel(
         def cell_moments(half):
             nc.vector.bn_aggr(out=c_mean_var[half][:], in_=c_stats[half][:].rearrange("p j s -> p (j s)"))
 
+        def gain_pairs_of_cell():
+            nc.gpsimd.tensor_copy(out=gain_pairs[:, :, 0], in_=gain_c)
+            nc.gpsimd.tensor_scalar(
+                out=gain_pairs[:, :, 1], in0=gain_c, scalar1=-1.0, scalar2=0.0, op0=ALU.mult, op1=ALU.add
+            )
+
         def cell_slope(half):
-            inverse_std(c_slope[half][:], c_mean_var[half][:, 1:2])
-            nc.gpsimd.tensor_tensor(
-                out=c_slope[half][:], in0=c_slope[half][:], in1=gain_c[:, half : half + 1], op=ALU.mult
+            inverse_std(c_inv[half][:], c_mean_var[half][:, 1:2])
+            nc.gpsimd.tensor_scalar(
+                out=c_pair[half][:], in0=gain_pairs[:, half, :], scalar1=c_inv[half][:], scalar2=0.0,
+                op0=ALU.mult, op1=ALU.add,
             )
-            nc.gpsimd.tensor_tensor(
-                out=c_shift[half][:], in0=c_slope[half][:], in1=c_mean_var[half][:, 0:1], op=ALU.mult
-            )
-            nc.gpsimd.tensor_tensor(
-                out=c_shift[half][:], in0=offset_c[:, half : half + 1], in1=c_shift[half][:], op=ALU.subtract
+            nc.gpsimd.tensor_scalar(
+                out=c_shift[half][:], in0=c_mean_var[half][:, 0:1], scalar1=c_pair[half][:, 1:2],
+                scalar2=offset_c[:, half : half + 1], op0=ALU.mult, op1=ALU.add,
             )
 
         def norm_cell(half, j, engine):
@@ -371,30 +363,37 @@ def tile_lstmcell_kernel(
             if engine == nc.scalar:
                 nc.scalar.activation(
                     out=c_next[half][:, chunk(j)], in_=raw[:, chunk(j)], func=ACT.Identity,
-                    scale=c_slope[half][:], bias=c_shift[half][:],
+                    scale=c_slope[half], bias=c_shift[half][:],
                 )
             else:
                 engine.tensor_scalar(
-                    out=c_next[half][:, chunk(j)], in0=raw[:, chunk(j)], scalar1=c_slope[half][:],
+                    out=c_next[half][:, chunk(j)], in0=raw[:, chunk(j)], scalar1=c_slope[half],
                     scalar2=c_shift[half][:], op0=ALU.mult, op1=ALU.add,
                 )
 
         def norm_whole_cell(half):
             nc.vector.tensor_scalar(
-                out=c_next[half][:], in0=gate[tile_of(FORGET, half)][:], scalar1=c_slope[half][:],
+                out=c_next[half][:], in0=gate[tile_of(FORGET, half)][:], scalar1=c_slope[half],
                 scalar2=c_shift[half][:], op0=ALU.mult, op1=ALU.add,
             )
 
         def tanh_cell(half, j):
             nc.scalar.activation(
                 out=tanh_c[half][:, chunk(j)], in_=gate[tile_of(FORGET, half)][:, chunk(j)], func=ACT.Tanh,
-                scale=c_slope[half][:], bias=c_shift[half][:],
+                scale=c_slope[half], bias=c_shift[half][:],
             )
 
         def gate_hidden(half, j, engine):
             h_next = gate[tile_of(OUT, half)]
             engine.tensor_tensor(
                 out=h_next[:, chunk(j)], in0=h_next[:, chunk(j)], in1=tanh_c[half][:, chunk(j)], op=ALU.mult
+            )
+
+        def keep_clock(src, first_column, reader):
+            unread = bank([P, CHUNK // 2], F32, reader)
+            nc.tensor.matmul(
+                out=unread[:], lhsT=ident_f32[:], rhs=src[:, first_column : first_column + CHUNK // 2],
+                start=True, stop=True,
             )
 
         def store(src, j, dram, half, reader):
@@ -537,28 +536,77 @@ def tile_lstmcell_kernel(
         PLAN(at, each_chunk, order.index, tile_of, take_new, keep_old, sum_cell, measure_cell, cell_moments, cell_slope,
              norm_cell, tanh_cell, gate_hidden, store, nc, gate, c_next, out_0, out_1, stage_hidden, store_hidden, norm_whole_cell)
 
-        for n in range(N_TILES + 4):
-            if n + 1 < N_TILES:
-                measure_input(n + 1)
-            if n + 2 < N_TILES:
-                hidden_outs(order[n + 2])
-            if 1 <= n <= N_TILES:
-                activate(order[n - 1], slice(0, BATCH // 2))
-            if n + 2 < N_TILES:
-                hidden_mean(order[n + 2])
-            if 1 <= n <= N_TILES:
-                activate(order[n - 1], slice(BATCH // 2, BATCH))
-            if n + 2 < N_TILES:
-                hidden_spread(order[n + 2])
+        FIRST, SECOND = slice(0, BATCH // 2), slice(BATCH // 2, BATCH)
+
+        def add_all(n, after_first):
+            for j in range(N_CHUNKS):
+                add_input(order[n], j)
+                if j == 0:
+                    after_first()
+                if j % 2 == 1 and n + 3 < N_TILES:
+                    hidden_chunk(order[n + 3], j // 2)
+
+        for n in range(5):
+            measure_input(n + 1)
+            hidden_outs(order[n + 2])
+            if n >= 1:
+                activate(order[n - 1], FIRST)
+            hidden_mean(order[n + 2])
+            if n >= 1:
+                activate(order[n - 1], SECOND)
+            hidden_spread(order[n + 2])
             run(n, "mid")
-            if n < N_TILES:
-                for j in range(N_CHUNKS):
-                    add_input(order[n], j)
-                    if j == 0:
-                        if n + 1 < N_TILES:
-                            input_moments(order[n + 1])
-                        weave(ratio_steps(order[n + 1]) if n + 1 < N_TILES else [], shift_steps(order[n]))
-                        run(n, "first")
-                    if j % 2 == 1 and n + 3 < N_TILES:
-                        hidden_chunk(order[n + 3], j // 2)
+            add_all(n, lambda: (input_moments(order[n + 1]), weave(ratio_steps(order[n + 1]), shift_steps(order[n]))))
             run(n, "end")
+            if n == 0:
+                gain_pairs_of_cell()
+
+        G, V = nc.gpsimd, nc.vector
+        measure_input(6)
+        hidden_outs(order[7])
+        activate(order[4], FIRST)
+        hidden_mean(order[7])
+        activate(order[4], SECOND)
+        hidden_spread(order[7])
+        for j in range(N_CHUNKS):
+            measure_cell(0, j)
+        cell_moments(0)
+        cell_slope(0)
+        add_all(5, lambda: (input_moments(order[6]), weave(ratio_steps(order[6]), shift_steps(order[5]))))
+        take_new(1, 0, G)
+        take_new(1, 1, G)
+        norm_whole_cell(0)
+        measure_input(7)
+        activate(order[5], FIRST)
+        activate(order[5], SECOND)
+        add_all(6, lambda: (input_moments(order[7]), weave(ratio_steps(order[7]), shift_steps(order[6]))))
+        for work in (lambda: keep_old(1, 0), lambda: keep_old(1, 1), lambda: sum_cell(1, 0, V), lambda: take_new(1, 2, V),
+                     lambda: sum_cell(1, 1, V), lambda: keep_old(1, 2), lambda: measure_cell(1, 0), lambda: take_new(1, 3, V),
+                     lambda: measure_cell(1, 1), lambda: keep_old(1, 3), lambda: sum_cell(1, 2, V), lambda: sum_cell(1, 3, V),
+                     lambda: measure_cell(1, 2), lambda: measure_cell(1, 3)):
+            work()
+        for j in range(N_CHUNKS):
+            store(c_next[0], j, out_0, 0, "s")
+        activate(order[6], FIRST)
+        activate(order[6], SECOND)
+        for j in range(N_CHUNKS):
+            tanh_cell(0, j)
+        add_all(7, lambda: (weave([], shift_steps(order[7])), cell_moments(1), cell_slope(1)))
+        activate(order[7], FIRST)
+        activate(order[7], SECOND)
+        for j in range(N_CHUNKS):
+            norm_cell(1, j, V)
+        for j in range(N_CHUNKS):
+            tanh_cell(1, j)
+            store(c_next[1], j, out_0, 1, "s")
+        h0, h1 = (lambda j: gate_hidden(0, j, V)), (lambda j: gate_hidden(1, j, V))
+        h0(0), h0(1), h1(0), h1(1)
+        stage_hidden(0, 0, "s"), stage_hidden(0, 1, "s")
+        h0(2), h0(3)
+        stage_hidden(1, 0, "v"), store_hidden(0)
+        h1(2)
+        stage_hidden(1, 1, "v"), store_hidden(1)
+        h1(3)
+        stage_hidden(0, 2, "s"), stage_hidden(0, 3, "s")
+        stage_hidden(1, 2, "v"), store_hidden(2)
+        stage_hidden(1, 3, "v"), store_hidden(3)

@@ -509,7 +509,9 @@ def tile_lstmcell_kernel(
         def measure_input(n):
             for j in range(1, N_CHUNKS):
                 input_stats(order[n], j)
-                if j < N_CHUNKS - 1 and n + 1 < N_TILES and n >= 1:
+                if n + 1 < N_TILES and n >= 2:
+                    hidden_chunk(order[n + 1], j)
+                elif j < N_CHUNKS - 1 and n == 1:
                     hidden_chunk(order[n + 1], j + 1)
 
         def half_at(n):
@@ -543,8 +545,8 @@ def tile_lstmcell_kernel(
                 add_input(order[n], j)
                 if j == 0:
                     after_first()
-                if j % 2 == 1 and n + 3 < N_TILES:
-                    hidden_chunk(order[n + 3], j // 2)
+                if j == 1 and n + 3 < N_TILES:
+                    hidden_chunk(order[n + 3], 0)
 
         for n in range(5):
             measure_input(n + 1)

@@ -166,17 +166,17 @@ def tile_lstmcell_kernel(
                 in_=grouped[:, 4 * j * CHUNK : 4 * (j + 1) * CHUNK],
             )
 
-        whhT = keep.tile([P, K_TILES, N_GATES], BF16, name="whhT")
-        hT = keep.tile([P, K_TILES, BATCH], BF16, name="hT")
+        whhT = keep.tile([P, N_GATES], F32, name="whhT")
+        hT = keep.tile([P, BATCH], F32, name="hT")
+        whhT_k = whhT[:].bitcast(BF16).rearrange("p (n e) -> p n e", e=K_TILES)
+        hT_k = hT[:].bitcast(BF16).rearrange("p (col e) -> p col e", e=K_TILES)
 
-        def transpose_rows(dst, src, j, readers):
-            for kt in range(K_TILES):
-                ps = bank([P, CHUNK], BF16, readers[kt])
-                for i in range(TILES_PER_CHUNK):
-                    nc.tensor.transpose(
-                        ps[:, i * P : (i + 1) * P], src[:, j * TILES_PER_CHUNK + i, kt * P : (kt + 1) * P], ident_bf[:]
-                    )
-                copy_out(readers[kt], dst[:, kt, chunk(j)], ps[:])
+        def transpose_rows(dst, src, j, reader):
+            words = src[:].rearrange("p t k -> p (t k)").bitcast(F32).rearrange("p (t w) -> p t w", w=P)
+            ps = bank([P, CHUNK], F32, reader)
+            for i in range(TILES_PER_CHUNK):
+                nc.tensor.transpose(ps[:, i * P : (i + 1) * P], words[:, j * TILES_PER_CHUNK + i, :], ident_f32[:])
+            copy_out(reader, dst[:, chunk(j)], ps[:])
 
         gate = [keep.tile([P, BATCH], F32, name="gate%d" % ft) for ft in range(N_TILES)]
         moments = [keep.tile([P, 2, 8], F32, name="moments%d" % ft) for ft in range(N_TILES)]
@@ -212,8 +212,8 @@ def tile_lstmcell_kernel(
                 hh_banks[(ft, j)] = bank([P, CHUNK], F32, hh_reader[(ft, j)])
             nc.tensor.matmul(
                 out=hh_banks[(ft, j)][:],
-                lhsT=whhT[:, kt, ft * P : (ft + 1) * P],
-                rhs=hT[:, kt, chunk(j)],
+                lhsT=whhT_k[:, ft * P : (ft + 1) * P, kt],
+                rhs=hT_k[:, chunk(j), kt],
                 start=(kt == 0),
                 stop=(kt == K_TILES - 1),
             )
@@ -447,18 +447,18 @@ def tile_lstmcell_kernel(
             hidden_chunk(order[n], j)
             hidden_out(order[n], j)
 
-        transpose_rows(whhT, whh_sb, 0, "vs")
-        transpose_rows(hT, h_sb, 0, "vs")
+        transpose_rows(whhT, whh_sb, 0, "v")
+        transpose_rows(hT, h_sb, 0, "s")
         transpose_x(0, "vs")
         whole_chunk(0, 0)
         quantise_x(0)
-        transpose_rows(hT, h_sb, 1, "vs")
-        transpose_rows(whhT, whh_sb, 1, "vs")
+        transpose_rows(hT, h_sb, 1, "s")
+        transpose_rows(whhT, whh_sb, 1, "v")
         first_stats(0)
         first_stats(1)
         whole_chunk(0, 1)
-        transpose_rows(hT, h_sb, 2, "vs")
-        transpose_rows(hT, h_sb, 3, "vs")
+        transpose_rows(hT, h_sb, 2, "s")
+        transpose_rows(hT, h_sb, 3, "v")
         first_stats(2)
         first_stats(3)
         whole_chunk(0, 2)

@@ -33,9 +33,11 @@ FORGET, IN, OUT, CELL = 0, 1, 2, 3
 
 BANKS = {"v": 4, "s": 4}
 
-HH_CHUNKS_ON_VECTOR = 1
+HH_CHUNKS_ON_VECTOR = [0, 0, 1, 1, 1, 1, 1, 0]
 
 WARM_UP_PASSES = 5
+
+SORTED_CHUNK = 1
 
 ORDER = [(IN, 0), (CELL, 0), (FORGET, 0), (IN, 1), (CELL, 1), (FORGET, 1), (OUT, 0), (OUT, 1)]
 
@@ -141,6 +143,13 @@ def tile_lstmcell_kernel(
         xq_codes = keep.tile([P, BATCH], U32, name="xq_codes", align_bytes=64)
         xq_plane = keep.tile([P, BATCH], U8, name="xq_plane", align_bytes=64)
 
+        x_sorted = keep.tile([P, TILES_PER_CHUNK, 2, P], F32, name="x_sorted")
+
+        def sort_x():
+            tiles = slice(SORTED_CHUNK * TILES_PER_CHUNK, (SORTED_CHUNK + 1) * TILES_PER_CHUNK)
+            src = x_words.rearrange("p (t q u) -> p t u q", t=ROW_TILES, u=2)
+            nc.scalar.copy(out=x_sorted[:], in_=src[:, tiles, :, :])
+
         def transpose_x(j, readers):
             for pair in range(TILES_PER_CHUNK // 2):
                 first = j * TILES_PER_CHUNK + 2 * pair
@@ -150,7 +159,8 @@ def tile_lstmcell_kernel(
                         base = (first + i) * words_per_row
                         nc.tensor.transpose(
                             xt[:, u, i * P : (i + 1) * P],
-                            x_words[:, base + u : base + words_per_row : 2],
+                            x_sorted[:, 2 * pair + i, u, :] if j == SORTED_CHUNK
+                            else x_words[:, base + u : base + words_per_row : 2],
                             ident_f32[:],
                         )
                 copy_out(
@@ -426,7 +436,7 @@ def tile_lstmcell_kernel(
 
         for n in range(N_TILES):
             for j in range(N_CHUNKS):
-                hh_reader[(order[n], j)] = "v" if (n >= 2 and j >= N_CHUNKS - HH_CHUNKS_ON_VECTOR) else "s"
+                hh_reader[(order[n], j)] = "v" if j >= N_CHUNKS - HH_CHUNKS_ON_VECTOR[n] else "s"
 
         def hidden_chunk(ft, j):
             for kt in range(K_TILES):
@@ -461,6 +471,7 @@ def tile_lstmcell_kernel(
         transpose_rows(hT, h_sb, 3, "v")
         first_stats(2)
         first_stats(3)
+        sort_x()
         whole_chunk(0, 2)
         whole_chunk(0, 3)
         whole_chunk(1, 0)
@@ -582,11 +593,20 @@ def tile_lstmcell_kernel(
         activate(order[5], FIRST)
         activate(order[5], SECOND)
         add_all(6, lambda: (input_moments(order[7]), weave(ratio_steps(order[7]), shift_steps(order[6]))))
-        for work in (lambda: keep_old(1, 0), lambda: keep_old(1, 1), lambda: sum_cell(1, 0, V), lambda: take_new(1, 2, V),
-                     lambda: sum_cell(1, 1, V), lambda: keep_old(1, 2), lambda: measure_cell(1, 0), lambda: take_new(1, 3, V),
-                     lambda: measure_cell(1, 1), lambda: keep_old(1, 3), lambda: sum_cell(1, 2, V), lambda: sum_cell(1, 3, V),
-                     lambda: measure_cell(1, 2), lambda: measure_cell(1, 3)):
-            work()
+        keep_old(1, 0)
+        keep_old(1, 1)
+        keep_old(1, 2)
+        keep_old(1, 3)
+        take_new(1, 2, V)
+        sum_cell(1, 0, V)
+        take_new(1, 3, V)
+        sum_cell(1, 1, V)
+        measure_cell(1, 0)
+        sum_cell(1, 2, V)
+        measure_cell(1, 1)
+        sum_cell(1, 3, V)
+        measure_cell(1, 2)
+        measure_cell(1, 3)
         for j in range(N_CHUNKS):
             store(c_next[0], j, out_0, 0, "s")
         activate(order[6], FIRST)

@@ -459,16 +459,16 @@ def tile_lstmcell_kernel(
 
         transpose_rows(whhT, whh_sb, 0, "v")
         transpose_rows(hT, h_sb, 0, "s")
-        transpose_x(0, "vs")
+        transpose_x(0, "sv")
         whole_chunk(0, 0)
         quantise_x(0)
         transpose_rows(hT, h_sb, 1, "s")
-        transpose_rows(whhT, whh_sb, 1, "v")
+        transpose_rows(whhT, whh_sb, 1, "s")
         first_stats(0)
         first_stats(1)
         whole_chunk(0, 1)
         transpose_rows(hT, h_sb, 2, "s")
-        transpose_rows(hT, h_sb, 3, "v")
+        transpose_rows(hT, h_sb, 3, "s")
         first_stats(2)
         first_stats(3)
         sort_x()

from contextlib import ExitStack
import math

import concourse.mybir as mybir
from concourse.masks import make_identity

F32 = mybir.dt.float32
BF16 = mybir.dt.bfloat16
I32 = mybir.dt.int32
U32 = mybir.dt.uint32
U8 = mybir.dt.uint8
FP8X4 = mybir.dt.float8_e4m3fn_x4
FP4X4 = mybir.dt.float4_e2m1fn_x4
ALU = mybir.AluOpType
ACT = mybir.ActivationFunctionType

P = 128
BATCH = 2048
N_IN = 512
N_HID = 256
N_GATES = 4 * N_HID
EPS = 1e-5
TINY_GAIN = 1e-18

CHUNK = 512
N_CHUNKS = BATCH // CHUNK
ROW_TILES = BATCH // P
TILES_PER_CHUNK = CHUNK // P
K_TILES = N_HID // P
HALVES = N_HID // P
N_TILES = N_GATES // P
FORGET, IN, OUT, CELL = 0, 1, 2, 3

BANKS = {"v": 4, "s": 4}

HH_CHUNKS_ON_VECTOR = [0, 0, 1, 1, 1, 1, 1, 0]

WARM_UP_PASSES = 5

SORTED_CHUNK = 1

ORDER = [(IN, 0), (CELL, 0), (FORGET, 0), (IN, 1), (CELL, 1), (FORGET, 1), (OUT, 0), (OUT, 1)]


def PLAN(at, each_chunk, pos, tile_of, take_new, keep_old, sum_cell, measure_cell, cell_moments, cell_slope,
         norm_cell, tanh_cell, gate_hidden, store, nc, gate, c_next, out_0, out_1, stage_hidden, store_hidden, norm_whole_cell):
    at(2, "end", lambda: each_chunk(lambda j: take_new(0, j, nc.gpsimd)))
    at(4, "mid", lambda: each_chunk(lambda j: keep_old(0, j), lambda j: sum_cell(0, j, nc.gpsimd)))


FLOPS = 2 * BATCH * N_GATES * (N_IN + N_HID)


def tile_lstmcell_kernel(
    tc, x, c, h, w_ih_words, w_ih_scales, w_hh, b, g_ih, b_ih, g_hh, b_hh, g_c, b_c, out_0, out_1
):
    nc = tc.nc
    with ExitStack() as ctx:
        ctx.enter_context(tc.manual_schedule())
        keep = ctx.enter_context(tc.tile_pool(name="keep", bufs=1))
        psum = ctx.enter_context(tc.psum_pool(name="psum", bufs=1))

        def bank(shape, dtype, reader):
            return psum.tile(shape, dtype, name="bank_" + reader, tag=reader, bufs=BANKS[reader])

        def chunk(j):
            return slice(j * CHUNK, (j + 1) * CHUNK)

        def copy_out(reader, out, in_):
            if reader == "v":
                nc.vector.tensor_copy(out=out, in_=in_)
            else:
                nc.scalar.copy(out=out, in_=in_)

        idle_work = keep.tile([P, CHUNK], BF16, name="idle_work")
        nc.vector.memset(idle_work[:], 0.0)
        for i in range(WARM_UP_PASSES):
            unread = bank([P, CHUNK], F32, "vs"[i % 2])
            nc.tensor.matmul(out=unread[:], lhsT=idle_work[:, 0:P], rhs=idle_work[:], start=True, stop=True)

        ident_bf = keep.tile([P, P], BF16, name="ident_bf")
        make_identity(nc, ident_bf[:])
        ident_f32 = keep.tile([P, P], F32, name="ident_f32")
        make_identity(nc, ident_f32[:])
        minus_half = keep.tile([P, 2], F32, name="minus_half")
        nc.vector.memset(minus_half[:], -0.5)
        minus_one = keep.tile([P, N_TILES], F32, name="minus_one")
        nc.vector.memset(minus_one[:], -1.0)
        eps2 = keep.tile([P, 2], F32, name="eps2")
        nc.vector.memset(eps2[:, 0:1], EPS)
        nc.vector.memset(eps2[:, 1:2], BATCH * EPS)
        warm = keep.tile([P, 1], F32, name="warm")
        nc.vector.memset(warm[:], 0.0)
        nc.scalar.activation(out=warm[:], in_=warm[:], func=ACT.Sigmoid)

        x_sb = keep.tile([P, ROW_TILES, N_IN], BF16, name="x_sb")
        x_rows = x.rearrange("(p t) k -> p t k", t=ROW_TILES)
        h_sb = keep.tile([P, ROW_TILES, N_HID], BF16, name="h_sb")
        h_rows = h.rearrange("(p t) k -> p t k", t=ROW_TILES)
        c_sb = keep.tile([P, ROW_TILES, N_HID], BF16, name="c_sb")
        c_rows = c.rearrange("(p t) k -> p t k", t=ROW_TILES)
        whh_sb = keep.tile([P, N_TILES, N_HID], BF16, name="whh_sb")
        whh_rows = w_hh.rearrange("(a p) k -> p a k", p=P)

        def load_chunk(dst, src, j):
            tiles = slice(j * TILES_PER_CHUNK, (j + 1) * TILES_PER_CHUNK)
            nc.sync.dma_start(out=dst[:, tiles, :], in_=src[:, tiles, :])

        par_rows = keep.tile([P, P], BF16, name="par_rows")
        nc.vector.memset(par_rows[:], 0.0)
        w_plane = keep.tile([P, N_GATES], U8, name="w_plane", align_bytes=64)
        nc.vector.memset(w_plane[:].bitcast(I32), 0)

        w_words = keep.tile([P, 2 * N_GATES], U8, name="w_words", align_bytes=64)
        load_chunk(whh_sb, whh_rows, 0)
        load_chunk(h_sb, h_rows, 0)
        load_chunk(x_sb, x_rows, 0)
        nc.sync.dma_start(out=w_words[:].bitcast(I32), in_=w_ih_words[0].bitcast(I32))
        for quad in range(4):
            nc.sync.dma_start(
                out=w_plane[32 * quad : 32 * quad + 4, :].bitcast(I32),
                in_=w_ih_scales[0, 4 * quad : 4 * quad + 4, :].bitcast(I32),
            )
        load_chunk(h_sb, h_rows, 1)
        load_chunk(whh_sb, whh_rows, 1)
        for j in range(2, N_CHUNKS):
            load_chunk(h_sb, h_rows, j)
        row = 0
        for vec in (g_ih, g_hh, b, b_ih, b_hh, g_c, b_c):
            n_rows = vec.shape[0] // P
            nc.sync.dma_start(out=par_rows[row : row + n_rows, :], in_=vec.rearrange("(a j) -> a j", j=P))
            row += n_rows
        n_par = row
        for j in range(1, N_CHUNKS):
            load_chunk(x_sb, x_rows, j)
        for j in range(N_CHUNKS):
            load_chunk(c_sb, c_rows, j)

        x_words = x_sb[:].rearrange("p t k -> p (t k)").bitcast(F32)
        words_per_row = N_IN // 2
        grouped = keep.tile([P, 4 * BATCH], BF16, name="grouped", align_bytes=64)
        grouped_words = grouped[:].bitcast(F32).rearrange("p (col u) -> p col u", u=2)
        xq_codes = keep.tile([P, BATCH], U32, name="xq_codes", align_bytes=64)
        xq_plane = keep.tile([P, BATCH], U8, name="xq_plane", align_bytes=64)

        x_sorted = keep.tile([P, TILES_PER_CHUNK, 2, P], F32, name="x_sorted")

        def sort_x():
            tiles = slice(SORTED_CHUNK * TILES_PER_CHUNK, (SORTED_CHUNK + 1) * TILES_PER_CHUNK)
            src = x_words.rearrange("p (t q u) -> p t u q", t=ROW_TILES, u=2)
            nc.scalar.copy(out=x_sorted[:], in_=src[:, tiles, :, :])

        def transpose_x(j, readers):
            for pair in range(TILES_PER_CHUNK // 2):
                first = j * TILES_PER_CHUNK + 2 * pair
                xt = bank([P, 2, 2 * P], F32, readers[pair])
                for u in range(2):
                    for i in range(2):
                        base = (first + i) * words_per_row
                        nc.tensor.transpose(
                            xt[:, u, i * P : (i + 1) * P],
                            x_sorted[:, 2 * pair + i, u, :] if j == SORTED_CHUNK
                            else x_words[:, base + u : base + words_per_row : 2],
                            ident_f32[:],
                        )
                copy_out(
                    readers[pair],
                    grouped_words[:, first * P : (first + 2) * P, :],
                    xt[:].rearrange("p u col -> p col u"),
                )

        def quantise_x(j):
            nc.vector.quantize_mx(
                out=xq_codes[:, chunk(j)].bitcast(FP8X4),
                scales=xq_plane[:, chunk(j)],
                in_=grouped[:, 4 * j * CHUNK : 4 * (j + 1) * CHUNK],
            )

        whhT = keep.tile([P, N_GATES], F32, name="whhT")
        hT = keep.tile([P, BATCH], F32, name="hT")
        whhT_k = whhT[:].bitcast(BF16).rearrange("p (n e) -> p n e", e=K_TILES)
        hT_k = hT[:].bitcast(BF16).rearrange("p (col e) -> p col e", e=K_TILES)

        def transpose_rows(dst, src, j, reader):
            words = src[:].rearrange("p t k -> p (t k)").bitcast(F32).rearrange("p (t w) -> p t w", w=P)
            ps = bank([P, CHUNK], F32, reader)
            for i in range(TILES_PER_CHUNK):
                nc.tensor.transpose(ps[:, i * P : (i + 1) * P], words[:, j * TILES_PER_CHUNK + i, :], ident_f32[:])
            copy_out(reader, dst[:, chunk(j)], ps[:])

        gate = [keep.tile([P, BATCH], F32, name="gate%d" % ft) for ft in range(N_TILES)]
        moments = [keep.tile([P, 2, 8], F32, name="moments%d" % ft) for ft in range(N_TILES)]
        stats = [keep.tile([P, N_CHUNKS, 6], F32, name="stats%d" % ft) for ft in range(N_TILES)]
        sums = [keep.tile([P, 16], F32, name="sums%d" % ft) for ft in range(N_TILES)]
        spread = [keep.tile([P, 2], F32, name="spread%d" % ft) for ft in range(N_TILES)]
        inv_std = [keep.tile([P, 2], F32, name="inv_std%d" % ft) for ft in range(N_TILES)]
        slope = [keep.tile([P, 2], F32, name="slope%d" % ft) for ft in range(N_TILES)]
        ratio = [keep.tile([P, 1], F32, name="ratio%d" % ft) for ft in range(N_TILES)]
        centre = [keep.tile([P, 1], F32, name="centre%d" % ft) for ft in range(N_TILES)]
        shift = [keep.tile([P, 1], F32, name="shift%d" % ft) for ft in range(N_TILES)]
        squares = keep.tile([P, BATCH], BF16, name="squares")
        scrap = keep.tile([P, N_CHUNKS], F32, name="scrap")
        hh_banks = {}
        hh_reader = {}

        def input_product(ft, j):
            ih = bank([P, CHUNK], F32, "v")
            nc.tensor.matmul_mx(
                out=ih[:],
                lhsT=w_words[:, 2 * ft * P : 2 * (ft + 1) * P].bitcast(FP4X4),
                lhsT_scale=w_plane[:, ft * P : (ft + 1) * P],
                rhs=xq_codes[:, chunk(j)].bitcast(FP8X4),
                rhs_scale=xq_plane[:, chunk(j)],
                start=True,
                stop=True,
            )
            return ih

        def hidden_pass(ft, i):
            j, kt = i // K_TILES, i % K_TILES
            if kt == 0:
                hh_banks[(ft, j)] = bank([P, CHUNK], F32, hh_reader[(ft, j)])
            nc.tensor.matmul(
                out=hh_banks[(ft, j)][:],
                lhsT=whhT_k[:, ft * P : (ft + 1) * P, kt],
                rhs=hT_k[:, chunk(j), kt],
                start=(kt == 0),
                stop=(kt == K_TILES - 1),
            )

        def hidden_out(ft, j):
            total = sums[ft][:, 4 + j : 5 + j]
            if hh_reader[(ft, j)] == "s":
                nc.scalar.activation(
                    out=gate[ft][:, chunk(j)], in_=hh_banks[(ft, j)][:], func=ACT.Identity, accum_out=total
                )
            else:
                nc.vector.tensor_scalar(
                    out=gate[ft][:, chunk(j)], in0=hh_banks[(ft, j)][:], scalar1=1.0, scalar2=None,
                    op0=ALU.mult, op1=ALU.add, accum_out=total,
                )

        def hidden_mean(ft):
            nc.scalar.activation(
                out=scrap[:], in_=sums[ft][:, 4 : 4 + N_CHUNKS], func=ACT.Identity,
                scale=-1.0 / BATCH, accum_out=moments[ft][:, 1, 0:1],
            )

        def hidden_spread(ft):
            nc.scalar.activation(
                out=squares[:], in_=gate[ft][:], func=ACT.Square, bias=moments[ft][:, 1, 0:1],
                accum_out=moments[ft][:, 1, 1:2],
            )

        def input_stats(ft, j):
            ih = input_product(ft, j)
            nc.vector.bn_stats(out=stats[ft][:, j, :], in_=ih[:])

        def input_moments(ft):
            nc.vector.bn_aggr(out=moments[ft][:, 0, 0:2], in_=stats[ft][:].rearrange("p j s -> p (j s)"))

        def inverse_std(out, variances):
            width = out.shape[1]
            nc.gpsimd.tensor_tensor(out=out, in0=variances, in1=eps2[:, 0:width], op=ALU.add)
            nc.gpsimd.tensor_tensor(out=out, in0=out, in1=minus_half[:, 0:width], op=ALU.pow)

        def ratio_steps(ft):
            return [
                lambda: nc.gpsimd.tensor_tensor(out=spread[ft][:], in0=moments[ft][:, :, 1], in1=eps2[:], op=ALU.add),
                lambda: nc.gpsimd.tensor_tensor(out=inv_std[ft][:], in0=spread[ft][:], in1=minus_half[:], op=ALU.pow),
                lambda: nc.gpsimd.tensor_tensor(
                    out=slope[ft][:], in0=inv_std[ft][:], in1=by_vec[:, 0:2, ft], op=ALU.mult
                ),
                lambda: nc.gpsimd.tensor_scalar(
                    out=ratio[ft][:], in0=slope[ft][:, 0:1], scalar1=spread[ft][:, 1:2],
                    scalar2=inv_std[ft][:, 1:2], op0=ALU.mult, op1=ALU.mult,
                ),
            ]

        def shift_steps(ft):
            return [
                lambda: nc.gpsimd.tensor_scalar(
                    out=centre[ft][:], in0=moments[ft][:, 0, 0:1], scalar1=ratio[ft][:],
                    scalar2=moments[ft][:, 1, 0:1], op0=ALU.mult, op1=ALU.subtract,
                ),
                lambda: nc.gpsimd.tensor_tensor(
                    out=centre[ft][:], in0=centre[ft][:], in1=slope[ft][:, 1:2], op=ALU.mult
                ),
                lambda: nc.gpsimd.tensor_tensor(
                    out=shift[ft][:], in0=offsets[:, ft : ft + 1], in1=centre[ft][:], op=ALU.subtract
                ),
            ]

        def weave(first, second):
            for i in range(max(len(first), len(second))):
                for steps in (first, second):
                    if i < len(steps):
                        steps[i]()

        def add_input(ft, j):
            ih = input_product(ft, j)
            nc.vector.scalar_tensor_tensor(
                out=gate[ft][:, chunk(j)], in0=ih[:], scalar=ratio[ft][:], in1=gate[ft][:, chunk(j)],
                op0=ALU.mult, op1=ALU.add,
            )

        def activate(ft, cols=slice(0, BATCH)):
            func = ACT.Tanh if ft // HALVES == CELL else ACT.Sigmoid
            nc.scalar.activation(
                out=gate[ft][:, cols], in_=gate[ft][:, cols], func=func, scale=slope[ft][:, 1:2], bias=shift[ft][:]
            )

        tanh_c = [keep.tile([P, BATCH], F32, name="tanh_c%d" % half) for half in range(HALVES)]
        c_next = [keep.tile([P, BATCH], F32, name="c_next%d" % half) for half in range(HALVES)]
        c_stats = [keep.tile([P, N_CHUNKS, 6], F32, name="c_stats%d" % half) for half in range(HALVES)]
        c_mean_var = [keep.tile([P, 2], F32, name="c_mean_var%d" % half) for half in range(HALVES)]
        c_inv = [keep.tile([P, 1], F32, name="c_inv%d" % half) for half in range(HALVES)]
        c_pair = [keep.tile([P, 2], F32, name="c_pair%d" % half) for half in range(HALVES)]
        c_slope = [c_pair[half][:, 0:1] for half in range(HALVES)]
        gain_pairs = keep.tile([P, HALVES, 2], F32, name="gain_pairs")
        c_shift = [keep.tile([P, 1], F32, name="c_shift%d" % half) for half in range(HALVES)]

        def tile_of(kind, half):
            return HALVES * kind + half

        def keep_old(half, j):
            cT = bank([P, CHUNK], BF16, "v")
            for i in range(TILES_PER_CHUNK):
                nc.tensor.transpose(
                    cT[:, i * P : (i + 1) * P], c_sb[:, j * TILES_PER_CHUNK + i, half * P : (half + 1) * P], ident_bf[:]
                )
            forget = gate[tile_of(FORGET, half)]
            nc.vector.tensor_tensor(out=forget[:, chunk(j)], in0=forget[:, chunk(j)], in1=cT[:], op=ALU.mult)

        def take_new(half, j, engine):
            in_gate = gate[tile_of(IN, half)]
            engine.tensor_tensor(
                out=in_gate[:, chunk(j)], in0=in_gate[:, chunk(j)], in1=gate[tile_of(CELL, half)][:, chunk(j)],
                op=ALU.mult,
            )

        def sum_cell(half, j, engine):
            raw = gate[tile_of(FORGET, half)]
            engine.tensor_tensor(
                out=raw[:, chunk(j)], in0=raw[:, chunk(j)], in1=gate[tile_of(IN, half)][:, chunk(j)], op=ALU.add
            )

        def measure_cell(half, j):
            nc.vector.bn_stats(out=c_stats[half][:, j, :], in_=gate[tile_of(FORGET, half)][:, chunk(j)])

        def cell_moments(half):
            nc.vector.bn_aggr(out=c_mean_var[half][:], in_=c_stats[half][:].rearrange("p j s -> p (j s)"))

        def gain_pairs_of_cell():
            nc.gpsimd.tensor_copy(out=gain_pairs[:, :, 0], in_=gain_c)
            nc.gpsimd.tensor_scalar(
                out=gain_pairs[:, :, 1], in0=gain_c, scalar1=-1.0, scalar2=0.0, op0=ALU.mult, op1=ALU.add
            )

        def cell_slope(half):
            inverse_std(c_inv[half][:], c_mean_var[half][:, 1:2])
            nc.gpsimd.tensor_scalar(
                out=c_pair[half][:], in0=gain_pairs[:, half, :], scalar1=c_inv[half][:], scalar2=0.0,
                op0=ALU.mult, op1=ALU.add,
            )
            nc.gpsimd.tensor_scalar(
                out=c_shift[half][:], in0=c_mean_var[half][:, 0:1], scalar1=c_pair[half][:, 1:2],
                scalar2=offset_c[:, half : half + 1], op0=ALU.mult, op1=ALU.add,
            )

        def norm_cell(half, j, engine):
            raw = gate[tile_of(FORGET, half)]
            if engine == nc.scalar:
                nc.scalar.activation(
                    out=c_next[half][:, chunk(j)], in_=raw[:, chunk(j)], func=ACT.Identity,
                    scale=c_slope[half], bias=c_shift[half][:],
                )
            else:
                engine.tensor_scalar(
                    out=c_next[half][:, chunk(j)], in0=raw[:, chunk(j)], scalar1=c_slope[half],
                    scalar2=c_shift[half][:], op0=ALU.mult, op1=ALU.add,
                )

        def norm_whole_cell(half):
            nc.vector.tensor_scalar(
                out=c_next[half][:], in0=gate[tile_of(FORGET, half)][:], scalar1=c_slope[half],
                scalar2=c_shift[half][:], op0=ALU.mult, op1=ALU.add,
            )

        def tanh_cell(half, j):
            nc.scalar.activation(
                out=tanh_c[half][:, chunk(j)], in_=gate[tile_of(FORGET, half)][:, chunk(j)], func=ACT.Tanh,
                scale=c_slope[half], bias=c_shift[half][:],
            )

        def gate_hidden(half, j, engine):
            h_next = gate[tile_of(OUT, half)]
            engine.tensor_tensor(
                out=h_next[:, chunk(j)], in0=h_next[:, chunk(j)], in1=tanh_c[half][:, chunk(j)], op=ALU.mult
            )

        def keep_clock(src, first_column, reader):
            unread = bank([P, CHUNK // 2], F32, reader)
            nc.tensor.matmul(
                out=unread[:], lhsT=ident_f32[:], rhs=src[:, first_column : first_column + CHUNK // 2],
                start=True, stop=True,
            )

        def store(src, j, dram, half, reader):
            ps = bank([P, TILES_PER_CHUNK, P], F32, reader)
            for i in range(TILES_PER_CHUNK):
                t = j * TILES_PER_CHUNK + i
                nc.tensor.transpose(ps[:, i, :], src[:, t * P : (t + 1) * P], ident_f32[:])
            rows = dram.rearrange("(p t) f -> p t f", t=ROW_TILES)
            tiles = slice(j * TILES_PER_CHUNK, (j + 1) * TILES_PER_CHUNK)
            staged = keep.tile([P, TILES_PER_CHUNK, P], F32, name="staged", tag="staged", bufs=8)
            copy_out(reader, staged[:], ps[:])
            nc.sync.dma_start(out=rows[:, tiles, half * P : (half + 1) * P], in_=staged[:])

        h_staged = {}

        def stage_hidden(half, j, reader):
            if j not in h_staged:
                h_staged[j] = keep.tile([P, TILES_PER_CHUNK, N_HID], F32, name="h_staged%d" % j)
            ps = bank([P, TILES_PER_CHUNK, P], F32, reader)
            for i in range(TILES_PER_CHUNK):
                t = j * TILES_PER_CHUNK + i
                nc.tensor.transpose(ps[:, i, :], gate[tile_of(OUT, half)][:, t * P : (t + 1) * P], ident_f32[:])
            copy_out(reader, h_staged[j][:, :, half * P : (half + 1) * P], ps[:])

        def store_hidden(j):
            rows = out_1.rearrange("(p t) f -> p t f", t=ROW_TILES)
            nc.sync.dma_start(out=rows[:, j * TILES_PER_CHUNK : (j + 1) * TILES_PER_CHUNK, :], in_=h_staged[j][:])

        order = [tile_of(kind, half) for kind, half in ORDER]

        for n in range(N_TILES):
            for j in range(N_CHUNKS):
                hh_reader[(order[n], j)] = "v" if j >= N_CHUNKS - HH_CHUNKS_ON_VECTOR[n] else "s"

        def hidden_chunk(ft, j):
            for kt in range(K_TILES):
                hidden_pass(ft, K_TILES * j + kt)
            if hh_reader[(ft, j)] == "v":
                hidden_out(ft, j)

        def hidden_outs(ft):
            for j in range(N_CHUNKS):
                if hh_reader[(ft, j)] == "s" and not (ft == order[2] and j < 2):
                    hidden_out(ft, j)

        def first_stats(pair):
            for n in (2 * pair, 2 * pair + 1):
                input_stats(order[n], 0)

        def whole_chunk(n, j):
            hidden_chunk(order[n], j)
            hidden_out(order[n], j)

        transpose_rows(whhT, whh_sb, 0, "v")
        transpose_rows(hT, h_sb, 0, "s")
        transpose_x(0, "sv")
        whole_chunk(0, 0)
        quantise_x(0)
        transpose_rows(hT, h_sb, 1, "s")
        transpose_rows(whhT, whh_sb, 1, "s")
        first_stats(0)
        first_stats(1)
        whole_chunk(0, 1)
        transpose_rows(hT, h_sb, 2, "s")
        transpose_rows(hT, h_sb, 3, "s")
        first_stats(2)
        first_stats(3)
        sort_x()
        whole_chunk(0, 2)
        whole_chunk(0, 3)
        whole_chunk(1, 0)
        hidden_mean(order[0])
        whole_chunk(1, 1)
        hidden_spread(order[0])
        par_ps = bank([P, P], BF16, "v")
        nc.tensor.transpose(par_ps[:], par_rows[:], ident_bf[:])
        par = keep.tile([P, n_par], F32, name="par")
        nc.vector.tensor_copy(out=par[:], in_=par_ps[:, 0:n_par])
        by_vec = par[:, 0 : 5 * N_TILES].rearrange("p (v a) -> p v a", a=N_TILES)
        gain_c = par[:, 5 * N_TILES : 5 * N_TILES + HALVES]
        offset_c = par[:, 5 * N_TILES + HALVES : 5 * N_TILES + 2 * HALVES]
        offsets = keep.tile([P, N_TILES], F32, name="offsets")
        nc.gpsimd.tensor_tensor(out=offsets[:], in0=by_vec[:, 2, :], in1=by_vec[:, 3, :], op=ALU.add)
        small = keep.tile([P, N_TILES], F32, name="small")
        nc.gpsimd.tensor_tensor(out=small[:], in0=by_vec[:, 1, :], in1=by_vec[:, 1, :], op=ALU.mult)
        nc.gpsimd.tensor_tensor(out=offsets[:], in0=offsets[:], in1=by_vec[:, 4, :], op=ALU.add)
        nc.gpsimd.tensor_scalar(
            out=small[:], in0=small[:], scalar1=TINY_GAIN * TINY_GAIN, scalar2=TINY_GAIN, op0=ALU.is_lt, op1=ALU.mult
        )
        nc.gpsimd.tensor_tensor(out=small[:], in0=by_vec[:, 1, :], in1=small[:], op=ALU.add)
        nc.gpsimd.tensor_scalar(
            out=by_vec[:, 1, :], in0=small[:], scalar1=math.sqrt(BATCH), scalar2=0.0, op0=ALU.mult, op1=ALU.add
        )
        nc.gpsimd.tensor_tensor(out=small[:], in0=by_vec[:, 1, :], in1=by_vec[:, 1, :], op=ALU.mult)
        nc.gpsimd.tensor_tensor(out=small[:], in0=small[:], in1=minus_one[:], op=ALU.pow)
        nc.gpsimd.tensor_tensor(out=small[:], in0=small[:], in1=by_vec[:, 1, :], op=ALU.mult)
        nc.gpsimd.tensor_tensor(out=by_vec[:, 0, :], in0=by_vec[:, 0, :], in1=small[:], op=ALU.mult)

        transpose_x(1, "vv")
        transpose_x(2, "vv")
        quantise_x(1)
        whole_chunk(1, 2)
        transpose_x(3, "vv")
        quantise_x(2)
        whole_chunk(1, 3)
        hidden_chunk(order[2], 0)
        hidden_out(order[2], 0)
        hidden_mean(order[1])
        hidden_chunk(order[2], 1)
        hidden_out(order[2], 1)
        hidden_spread(order[1])
        quantise_x(3)

        def measure_input(n):
            for j in range(1, N_CHUNKS):
                input_stats(order[n], j)
                if n + 1 < N_TILES and n >= 2:
                    hidden_chunk(order[n + 1], j)
                elif j < N_CHUNKS - 1 and n == 1:
                    hidden_chunk(order[n + 1], j + 1)

        def half_at(n):
            return order[n] % HALVES

        measure_input(0)
        input_moments(order[0])
        weave(ratio_steps(order[0]), [])

        def each_chunk(*stages):
            for j in range(N_CHUNKS):
                for stage in stages:
                    stage(j)

        plan = {}

        def at(step, slot, work):
            plan.setdefault((step, slot), []).append(work)

        def run(step, slot):
            for work in plan.get((step, slot), []):
                work()

        PLAN(at, each_chunk, order.index, tile_of, take_new, keep_old, sum_cell, measure_cell, cell_moments, cell_slope,
             norm_cell, tanh_cell, gate_hidden, store, nc, gate, c_next, out_0, out_1, stage_hidden, store_hidden, norm_whole_cell)

        FIRST, SECOND = slice(0, BATCH // 2), slice(BATCH // 2, BATCH)

        def add_all(n, after_first):
            for j in range(N_CHUNKS):
                add_input(order[n], j)
                if j == 0:
                    after_first()
                if j == 1 and n + 3 < N_TILES:
                    hidden_chunk(order[n + 3], 0)

        for n in range(5):
            measure_input(n + 1)
            hidden_outs(order[n + 2])
            if n >= 1:
                activate(order[n - 1], FIRST)
            hidden_mean(order[n + 2])
            if n >= 1:
                activate(order[n - 1], SECOND)
            hidden_spread(order[n + 2])
            run(n, "mid")
            add_all(n, lambda: (input_moments(order[n + 1]), weave(ratio_steps(order[n + 1]), shift_steps(order[n]))))
            run(n, "end")
            if n == 0:
                gain_pairs_of_cell()

        G, V = nc.gpsimd, nc.vector
        measure_input(6)
        hidden_outs(order[7])
        activate(order[4], FIRST)
        hidden_mean(order[7])
        activate(order[4], SECOND)
        hidden_spread(order[7])
        for j in range(N_CHUNKS):
            measure_cell(0, j)
        cell_moments(0)
        cell_slope(0)
        add_all(5, lambda: (input_moments(order[6]), weave(ratio_steps(order[6]), shift_steps(order[5]))))
        take_new(1, 0, G)
        take_new(1, 1, G)
        norm_whole_cell(0)
        measure_input(7)
        activate(order[5], FIRST)
        activate(order[5], SECOND)
        add_all(6, lambda: (input_moments(order[7]), weave(ratio_steps(order[7]), shift_steps(order[6]))))
        keep_old(1, 0)
        keep_old(1, 1)
        keep_old(1, 2)
        keep_old(1, 3)
        take_new(1, 2, V)
        sum_cell(1, 0, V)
        take_new(1, 3, V)
        sum_cell(1, 1, V)
        measure_cell(1, 0)
        sum_cell(1, 2, V)
        measure_cell(1, 1)
        sum_cell(1, 3, V)
        measure_cell(1, 2)
        measure_cell(1, 3)
        for j in range(N_CHUNKS):
            store(c_next[0], j, out_0, 0, "s")
        activate(order[6], FIRST)
        activate(order[6], SECOND)
        for j in range(N_CHUNKS):
            tanh_cell(0, j)
        add_all(7, lambda: (weave([], shift_steps(order[7])), cell_moments(1), cell_slope(1)))
        activate(order[7], FIRST)
        activate(order[7], SECOND)
        for j in range(N_CHUNKS):
            norm_cell(1, j, V)
        for j in range(N_CHUNKS):
            tanh_cell(1, j)
            store(c_next[1], j, out_0, 1, "s")
        h0, h1 = (lambda j: gate_hidden(0, j, V)), (lambda j: gate_hidden(1, j, V))
        h0(0), h0(1), h1(0), h1(1)
        stage_hidden(0, 0, "s"), stage_hidden(0, 1, "s")
        h0(2), h0(3)
        stage_hidden(1, 0, "v"), store_hidden(0)
        h1(2)
        stage_hidden(1, 1, "v"), store_hidden(1)
        h1(3)
        stage_hidden(0, 2, "s"), stage_hidden(0, 3, "s")
        stage_hidden(1, 2, "v"), store_hidden(2)
        stage_hidden(1, 3, "v"), store_hidden(3)
